import numpy as np
import ml_dtypes


def mxq(x, axis, fmt="e4m3"):
    dtype, down = {"e4m3": (ml_dtypes.float8_e4m3fn, 7), "e5m2": (ml_dtypes.float8_e5m2, 14)}[fmt]
    v = np.moveaxis(np.asarray(x, np.float32).astype(ml_dtypes.bfloat16).astype(np.float64), axis, -1)
    blocks = v.reshape(v.shape[:-1] + (-1, 32))
    amax = np.abs(blocks).max(-1, keepdims=True)
    byte = np.maximum(np.where(amax > 0, np.frexp(amax)[1] - 1 + 127, 0) - down, 1)
    scale = np.exp2(byte - 127.0)
    codes = (blocks / scale).astype(np.float32).astype(dtype).astype(np.float64)
    return np.moveaxis((codes * scale).reshape(v.shape), -1, axis)


WIDE = False


def mx_kscale(k):
    if not WIDE:
        return np.ones(k)
    levels = np.array([10, -10, 5, -5, 0])
    a = np.random.permutation(np.resize(levels, k // 512 * 4)).reshape(k // 512, 4)
    idx = np.arange(k)
    return np.exp2(a[idx // 512, idx % 128 // 32])


BF16 = ml_dtypes.bfloat16


def bf(x):
    return np.asarray(x, np.float32).astype(BF16)


def f64(x):
    return np.asarray(x).astype(np.float64)


E2M1 = np.array([0.0, 0.5, 1.0, 1.5, 2.0, 3.0, 4.0, 6.0, -0.0, -0.5, -1.0, -1.5, -2.0, -3.0, -4.0, -6.0])


def pack_weight(w, fmt):
    k, n = w.shape
    w = f64(bf(w)).reshape(k // 32, 32, n)
    amax = np.abs(w).max(1)
    if fmt == "e4m3":
        byte = np.frexp(amax)[1] - 1 + 127 - 7
    else:
        mant, ex = np.frexp(amax / 6.0)
        byte = np.where(mant > 0.5, ex, ex - 1) + 127
    byte = np.clip(np.where(amax > 0, byte, 1), 1, 254)
    scaled = (w * np.exp2(127.0 - byte)[:, None, :]).reshape(k, n).astype(np.float32)
    by_word = np.ascontiguousarray(scaled.reshape(k // 512, 128, 4, n).transpose(0, 1, 3, 2))
    if fmt == "e4m3":
        words = by_word.astype(ml_dtypes.float8_e4m3fn).view(np.uint8)
    else:
        c = by_word.astype(ml_dtypes.float4_e2m1fn).view(np.uint8) & 0xF
        words = c[..., 0::2] | (c[..., 1::2] << 4)
    return np.ascontiguousarray(words), np.ascontiguousarray(byte.astype(np.uint8).reshape(k // 512, 16, n))


def unpack_weight(words, scales, fmt):
    g, p, n, _ = words.shape
    if fmt == "e4m3":
        vals = np.ascontiguousarray(words).view(ml_dtypes.float8_e4m3fn).astype(np.float64)
    else:
        nib = np.empty((g, p, n, 4), np.uint8)
        nib[..., 0::2] = words & 0xF
        nib[..., 1::2] = words >> 4
        vals = E2M1[nib]
    vals = vals * np.repeat(np.exp2(scales.astype(np.float64) - 127.0), 8, axis=1)[..., None]
    return vals.transpose(0, 1, 3, 2).reshape(g * 512, n)


BS, BLOCK, HID, GAP, G = 256, 512, 1024, 64, 8


def elu(v):
    return np.where(v > 0.0, v, np.exp(np.minimum(v, 0.0)) - 1.0)


def setup_inputs():
    s = mx_kscale(BLOCK)
    s = s / s.max()
    y_lanes = bf((np.random.standard_normal((BS, BLOCK, G)) * 1.3 * s[None, :, None]).reshape(BS, BLOCK * G))
    w1 = np.random.standard_normal((G, BLOCK, HID)) / np.sqrt(BLOCK) / s[None, :, None]
    b1 = bf(np.random.standard_normal((G, 1, HID)) * 0.2)
    w2 = np.random.standard_normal((G, HID, BLOCK)) / np.sqrt(HID)
    b2 = bf(np.random.standard_normal((G, 1, BLOCK)) * 0.2)
    w1_words, w1_scales = pack_weight(w1.reshape(-1, HID), "e4m3")
    w2_words, w2_scales = pack_weight(w2.reshape(-1, BLOCK), "e4m3")
    return {"y_lanes": y_lanes,
            "w1_words": w1_words,
            "w1_scales": w1_scales,
            "b1": b1,
            "w2_words": w2_words,
            "w2_scales": w2_scales,
            "b2": b2}


def reference(y_lanes, w1_words, w1_scales, b1, w2_words, w2_scales, b2):
    y = f64(y_lanes)
    bs = y.shape[0]
    y = y.reshape(-1, BLOCK, G).transpose(0, 2, 1).reshape(bs, -1)
    z = y.reshape(bs, -1, BLOCK).transpose(1, 0, 2)
    h = elu((mxq(z, 2, "e4m3") @ unpack_weight(w1_words, w1_scales, "e4m3").reshape(G, BLOCK, HID)) + f64(b1))
    h = (mxq(h, 2, "e4m3") @ unpack_weight(w2_words, w2_scales, "e4m3").reshape(G, HID, BLOCK)) + f64(b2)
    z = h + z
    y = z.transpose(1, 0, 2).reshape(bs, -1)
    return y.reshape(-1, G, BLOCK).transpose(0, 2, 1).reshape(bs, -1)

@@ -1,0 +1,249 @@
+from contextlib import ExitStack
+
+import concourse.mybir as mybir
+from concourse.masks import make_identity
+
+F32 = mybir.dt.float32
+BF16 = mybir.dt.bfloat16
+I32 = mybir.dt.int32
+U32 = mybir.dt.uint32
+U8 = mybir.dt.uint8
+FP8X4 = mybir.dt.float8_e4m3fn_x4
+ALU = mybir.AluOpType
+ACT = mybir.ActivationFunctionType
+
+P = 128
+PACK = 4
+K_PASS = P * PACK
+LANES = 8
+BLOCK = 512
+HID = 1024
+ROWS = 256
+ROW_TILES = ROWS // P
+HID_PASSES = HID // K_PASS
+LANE_GROUP = 4
+GROUPS = LANES // LANE_GROUP
+FEAT_CHUNK = P
+FEAT_CHUNKS = BLOCK // FEAT_CHUNK
+WORD_LANES = 2
+QUADRANTS = 4
+
+FLOPS = 2 * LANES * ROWS * (BLOCK * HID + HID * BLOCK)
+
+
+def tile_blockresmlp_mixerblock_pa_e_kernel(
+    tc, y_lanes, w1_words, w1_scales, b1, w2_words, w2_scales, b2, out
+):
+    nc = tc.nc
+    with ExitStack() as ctx:
+        keep = ctx.enter_context(tc.tile_pool(name="keep", bufs=1))
+        work = ctx.enter_context(tc.tile_pool(name="work", bufs=2))
+        psum = ctx.enter_context(tc.psum_pool(name="psum", bufs=2))
+
+        ident = keep.tile([P, P], F32)
+        make_identity(nc, ident[:])
+        warm = keep.tile([P, 1], F32)
+        nc.vector.memset(warm[:], 0.0)
+        nc.scalar.activation(out=warm[:], in_=warm[:], func=ACT.Exp)
+
+        y_sb = [keep.tile([P, BLOCK * LANES], BF16, name="y%d" % r) for r in range(ROW_TILES)]
+        w1_codes = keep.tile([P, LANES, HID], U32, align_bytes=64)
+        w2_codes = keep.tile([P, LANES * HID_PASSES, BLOCK], U32, align_bytes=64)
+        w1_planes = keep.tile([P, GROUPS, HID], U8, align_bytes=64)
+        w2_planes = keep.tile([P, GROUPS * HID_PASSES, BLOCK], U8, align_bytes=64)
+        b1_all = keep.tile([P, LANES, HID], BF16)
+        b2_all = keep.tile([P, LANES, BLOCK], BF16)
+        result = [keep.tile([P, BLOCK, LANES], F32, name="result%d" % r) for r in range(ROW_TILES)]
+        z_grouped = [
+            keep.tile([P, LANES, P, PACK], BF16, name="z_grouped%d" % r, align_bytes=64)
+            for r in range(ROW_TILES)
+        ]
+        z_codes = [keep.tile([P, LANES, P], U32, name="z_codes%d" % r, align_bytes=64) for r in range(ROW_TILES)]
+        z_scales = [keep.tile([P, LANES, P], U8, name="z_scales%d" % r, align_bytes=64) for r in range(ROW_TILES)]
+        h_codes = [
+            keep.tile([P, LANES, HID_PASSES, P], U32, name="h_codes%d" % r, align_bytes=64)
+            for r in range(ROW_TILES)
+        ]
+        h_scales = [
+            keep.tile([P, LANES, HID_PASSES, P], U8, name="h_scales%d" % r, align_bytes=64)
+            for r in range(ROW_TILES)
+        ]
+
+        nc.vector.memset(w1_planes[:].bitcast(I32), 0)
+        nc.vector.memset(w2_planes[:].bitcast(I32), 0)
+
+        def load_y(r):
+            nc.sync.dma_start(out=y_sb[r][:], in_=y_lanes[r * P : (r + 1) * P, :])
+
+        def load_planes(planes, scales, tiles):
+            for j in range(tiles):
+                for quad in range(QUADRANTS):
+                    nc.sync.dma_start(
+                        out=planes[32 * quad : 32 * quad + 16, j, :].bitcast(I32),
+                        in_=scales[4 * j : 4 * j + 4, 4 * quad : 4 * quad + 4, :].bitcast(I32),
+                    )
+
+        def load_w1(g):
+            nc.sync.dma_start(
+                out=w1_codes[:, g, :].bitcast(I32),
+                in_=w1_words[g].rearrange("p n t -> p (n t)").bitcast(I32),
+            )
+
+        def load_w2(g):
+            passes = slice(g * HID_PASSES, (g + 1) * HID_PASSES)
+            nc.sync.dma_start(
+                out=w2_codes[:, passes, :].bitcast(I32),
+                in_=w2_words[passes].rearrange("c p n t -> p c (n t)").bitcast(I32),
+            )
+
+        load_y(0)
+        load_planes(w1_planes, w1_scales, GROUPS)
+        for g in range(LANE_GROUP):
+            load_w1(g)
+        load_y(1)
+        for g in range(LANE_GROUP, LANES):
+            load_w1(g)
+        load_planes(w2_planes, w2_scales, GROUPS * HID_PASSES)
+        for g in range(LANES):
+            load_w2(g)
+        for g in range(0, LANES, 2):
+            nc.scalar.dma_start(
+                out=b1_all[:, g : g + 2, :].rearrange("p g n -> p (g n)"),
+                in_=b1[g : g + 2].rearrange("g o n -> (g o n)").partition_broadcast(P),
+            )
+        nc.scalar.dma_start(
+            out=b2_all[:].rearrange("p g n -> p (g n)"),
+            in_=b2.rearrange("g o n -> (g o n)").partition_broadcast(P),
+        )
+
+        def residual_plus_bias(r):
+            for f in range(FEAT_CHUNKS):
+                feats = slice(f * FEAT_CHUNK, (f + 1) * FEAT_CHUNK)
+                nc.gpsimd.tensor_tensor(
+                    out=result[r][:, feats, :],
+                    in0=y_sb[r][:].rearrange("b (d g) -> b d g", g=LANES)[:, feats, :],
+                    in1=b2_all[:, :, feats].rearrange("b g d -> b d g"),
+                    op=ALU.add,
+                )
+
+        def transpose_z(r, pair):
+            y_words = y_sb[r][:].bitcast(F32)
+            words = BLOCK * LANES // WORD_LANES
+            step = PACK * LANES // WORD_LANES
+            zt = psum.tile([P, PACK, P], F32, tag="transposed", bufs=4)
+            for t in range(PACK):
+                first = t * LANES // WORD_LANES + pair
+                nc.tensor.transpose(zt[:, t, :], y_words[:, first:words:step], ident[:])
+            nc.scalar.copy(
+                out=z_grouped[r][:, WORD_LANES * pair : WORD_LANES * (pair + 1), :, :],
+                in_=zt[:].bitcast(BF16).rearrange("p t (b e) -> p e b t", e=WORD_LANES),
+            )
+
+        def quantise_z(r, group):
+            lanes = slice(group * LANE_GROUP, (group + 1) * LANE_GROUP)
+            nc.vector.quantize_mx(
+                out=z_codes[r][:, lanes, :].rearrange("p g b -> p (g b)").bitcast(FP8X4),
+                scales=z_scales[r][:, lanes, :].rearrange("p g b -> p (g b)"),
+                in_=z_grouped[r][:, lanes, :, :].rearrange("p g b t -> p (g b t)"),
+            )
+
+        def layer1(r, g):
+            sorted_sums = []
+            for c in range(HID_PASSES):
+                hid_cols = slice(c * K_PASS, (c + 1) * K_PASS)
+                acc1 = psum.tile([P, K_PASS], F32, tag="acc1", bufs=2)
+                nc.tensor.matmul_mx(
+                    out=acc1[:],
+                    lhsT=z_codes[r][:, g, :].bitcast(FP8X4),
+                    lhsT_scale=z_scales[r][:, g, :],
+                    rhs=w1_codes[:, g, hid_cols].bitcast(FP8X4),
+                    rhs_scale=w1_planes[4 * (g % LANE_GROUP) : P, g // LANE_GROUP, hid_cols],
+                    start=True,
+                    stop=True,
+                )
+                v = work.tile([P, PACK, P], F32, tag="v", bufs=4)
+                nc.vector.tensor_tensor(
+                    out=v[:],
+                    in0=acc1[:].rearrange("b (p t) -> b t p", t=PACK),
+                    in1=b1_all[:, g, hid_cols].rearrange("b (p t) -> b t p", t=PACK),
+                    op=ALU.add,
+                )
+                sorted_sums.append(v)
+            return sorted_sums
+
+        def elu_and_quantise(r, g, sorted_sums):
+            h_grouped = work.tile([P, HID_PASSES, P, PACK], BF16, tag="h_grouped", bufs=2, align_bytes=64)
+            for c in range(HID_PASSES):
+                vt = psum.tile([P, PACK, P], F32, tag="transposed", bufs=4)
+                for t in range(PACK):
+                    nc.tensor.transpose(vt[:, t, :], sorted_sums[c][:, t, :], ident[:])
+                v_by_word = vt[:].rearrange("p t b -> p b t")
+                gap = work.tile([P, P, PACK], F32, tag="gap", bufs=3)
+                nc.scalar.activation(out=gap[:], in_=v_by_word, func=ACT.Exp)
+                nc.scalar.activation(out=gap[:], in_=gap[:], func=ACT.Relu, scale=-1.0, bias=1.0)
+                nc.vector.scalar_tensor_tensor(
+                    out=h_grouped[:, c, :, :],
+                    in0=gap[:],
+                    scalar=-1.0,
+                    in1=v_by_word,
+                    op0=ALU.mult,
+                    op1=ALU.max,
+                )
+            nc.vector.quantize_mx(
+                out=h_codes[r][:, g, :, :].rearrange("p c b -> p (c b)").bitcast(FP8X4),
+                scales=h_scales[r][:, g, :, :].rearrange("p c b -> p (c b)"),
+                in_=h_grouped[:].rearrange("p c b t -> p (c b t)"),
+            )
+
+        def layer2(r, group):
+            for f in range(FEAT_CHUNKS):
+                feats = slice(f * FEAT_CHUNK, (f + 1) * FEAT_CHUNK)
+                acc2 = psum.tile([P, LANE_GROUP, FEAT_CHUNK], F32, tag="acc2", bufs=2)
+                for i in range(LANE_GROUP):
+                    g = group * LANE_GROUP + i
+                    for c in range(HID_PASSES):
+                        k_group = g * HID_PASSES + c
+                        nc.tensor.matmul_mx(
+                            out=acc2[:, i, :],
+                            lhsT=h_codes[r][:, g, c, :].bitcast(FP8X4),
+                            lhsT_scale=h_scales[r][:, g, c, :],
+                            rhs=w2_codes[:, k_group, feats].bitcast(FP8X4),
+                            rhs_scale=w2_planes[4 * (k_group % 4) : P, k_group // 4, feats],
+                            start=(c == 0),
+                            stop=(c == HID_PASSES - 1),
+                        )
+                lanes = slice(group * LANE_GROUP, (group + 1) * LANE_GROUP)
+                nc.vector.tensor_tensor(
+                    out=result[r][:, feats, lanes],
+                    in0=acc2[:].rearrange("b g d -> b d g"),
+                    in1=result[r][:, feats, lanes],
+                    op=ALU.add,
+                )
+                if group == GROUPS - 1:
+                    nc.sync.dma_start(
+                        out=out[r * P : (r + 1) * P, f * FEAT_CHUNK * LANES : (f + 1) * FEAT_CHUNK * LANES],
+                        in_=result[r][:, feats, :].rearrange("b d g -> b (d g)"),
+                    )
+
+        for pair in range(LANES // WORD_LANES):
+            transpose_z(0, pair)
+            if pair % 2 == 1:
+                quantise_z(0, pair // 2)
+        for r in range(ROW_TILES):
+            residual_plus_bias(r)
+
+        units = [(r, g) for r in range(ROW_TILES) for g in range(LANES)]
+        ahead = layer1(*units[0])
+        for i, (r, g) in enumerate(units):
+            sums = ahead
+            if r + 1 < ROW_TILES and g % 2 == 0:
+                transpose_z(r + 1, g // 2)
+                if g % 4 == 2:
+                    quantise_z(r + 1, g // 4)
+            if i + 1 < len(units):
+                ahead = layer1(*units[i + 1])
+            elu_and_quantise(r, g, sums)
+            if i > 0 and i % LANE_GROUP == 0:
+                done = i // LANE_GROUP - 1
+                layer2(done // GROUPS, done % GROUPS)
+        layer2(ROW_TILES - 1, GROUPS - 1)

@@ -26,7 +26,11 @@ GROUPS = LANES // LANE_GROUP
 FEAT_CHUNK = P
 FEAT_CHUNKS = BLOCK // FEAT_CHUNK
 WORD_LANES = 2
+PAIRS_PER_TILE = LANES // WORD_LANES
+K_STEP = PACK * PAIRS_PER_TILE
 QUADRANTS = 4
+PSUM_BANKS = 8
+L2_LAG = 7
 
 FLOPS = 2 * LANES * ROWS * (BLOCK * HID + HID * BLOCK)
 
@@ -38,7 +42,8 @@ def tile_blockresmlp_mixerblock_pa_e_kernel(
     with ExitStack() as ctx:
         keep = ctx.enter_context(tc.tile_pool(name="keep", bufs=1))
         work = ctx.enter_context(tc.tile_pool(name="work", bufs=2))
-        psum = ctx.enter_context(tc.psum_pool(name="psum", bufs=2))
+        psum = ctx.enter_context(tc.psum_pool(name="psum", bufs=PSUM_BANKS))
+        ctx.enter_context(tc.manual_schedule())
 
         ident = keep.tile([P, P], F32)
         make_identity(nc, ident[:])
@@ -54,10 +59,6 @@ def tile_blockresmlp_mixerblock_pa_e_kernel(
         b1_all = keep.tile([P, LANES, HID], BF16)
         b2_all = keep.tile([P, LANES, BLOCK], BF16)
         result = [keep.tile([P, BLOCK, LANES], F32, name="result%d" % r) for r in range(ROW_TILES)]
-        z_grouped = [
-            keep.tile([P, LANES, P, PACK], BF16, name="z_grouped%d" % r, align_bytes=64)
-            for r in range(ROW_TILES)
-        ]
         z_codes = [keep.tile([P, LANES, P], U32, name="z_codes%d" % r, align_bytes=64) for r in range(ROW_TILES)]
         z_scales = [keep.tile([P, LANES, P], U8, name="z_scales%d" % r, align_bytes=64) for r in range(ROW_TILES)]
         h_codes = [
@@ -83,11 +84,12 @@ def tile_blockresmlp_mixerblock_pa_e_kernel(
                         in_=scales[4 * j : 4 * j + 4, 4 * quad : 4 * quad + 4, :].bitcast(I32),
                     )
 
-        def load_w1(g):
+        def load_layer1(g):
             nc.sync.dma_start(
                 out=w1_codes[:, g, :].bitcast(I32),
                 in_=w1_words[g].rearrange("p n t -> p (n t)").bitcast(I32),
             )
+            nc.sync.dma_start(out=b1_all[:, g, :], in_=b1[g].rearrange("o n -> (o n)").partition_broadcast(P))
 
         def load_w2(g):
             passes = slice(g * HID_PASSES, (g + 1) * HID_PASSES)
@@ -99,22 +101,17 @@ def tile_blockresmlp_mixerblock_pa_e_kernel(
         load_y(0)
         load_planes(w1_planes, w1_scales, GROUPS)
         for g in range(LANE_GROUP):
-            load_w1(g)
-        load_y(1)
-        for g in range(LANE_GROUP, LANES):
-            load_w1(g)
-        load_planes(w2_planes, w2_scales, GROUPS * HID_PASSES)
-        for g in range(LANES):
-            load_w2(g)
-        for g in range(0, LANES, 2):
-            nc.scalar.dma_start(
-                out=b1_all[:, g : g + 2, :].rearrange("p g n -> p (g n)"),
-                in_=b1[g : g + 2].rearrange("g o n -> (g o n)").partition_broadcast(P),
-            )
-        nc.scalar.dma_start(
+            load_layer1(g)
+        nc.sync.dma_start(
             out=b2_all[:].rearrange("p g n -> p (g n)"),
             in_=b2.rearrange("g o n -> (g o n)").partition_broadcast(P),
         )
+        load_y(1)
+        for g in range(LANE_GROUP, LANES):
+            load_layer1(g)
+        load_planes(w2_planes, w2_scales, GROUPS * HID_PASSES)
+        for g in range(LANES):
+            load_w2(g)
 
         def residual_plus_bias(r):
             for f in range(FEAT_CHUNKS):
@@ -126,32 +123,34 @@ def tile_blockresmlp_mixerblock_pa_e_kernel(
                     op=ALU.add,
                 )
 
-        def transpose_z(r, pair):
+        def transpose_z(pair):
+            r, j = divmod(pair, PAIRS_PER_TILE)
             y_words = y_sb[r][:].bitcast(F32)
-            words = BLOCK * LANES // WORD_LANES
-            step = PACK * LANES // WORD_LANES
-            zt = psum.tile([P, PACK, P], F32, tag="transposed", bufs=4)
+            zt = psum.tile([P, PACK, P], F32, tag="bank")
             for t in range(PACK):
-                first = t * LANES // WORD_LANES + pair
-                nc.tensor.transpose(zt[:, t, :], y_words[:, first:words:step], ident[:])
+                first = t * PAIRS_PER_TILE + j
+                nc.tensor.transpose(zt[:, t, :], y_words[:, first : BLOCK * PAIRS_PER_TILE : K_STEP], ident[:])
+            z_grouped = work.tile([P, WORD_LANES, P, PACK], BF16, tag="z_grouped", bufs=2, align_bytes=64)
             nc.scalar.copy(
-                out=z_grouped[r][:, WORD_LANES * pair : WORD_LANES * (pair + 1), :, :],
+                out=z_grouped[:],
                 in_=zt[:].bitcast(BF16).rearrange("p t (b e) -> p e b t", e=WORD_LANES),
             )
+            return z_grouped
 
-        def quantise_z(r, group):
-            lanes = slice(group * LANE_GROUP, (group + 1) * LANE_GROUP)
+        def quantise_z(pair, z_grouped):
+            r, j = divmod(pair, PAIRS_PER_TILE)
+            lanes = slice(j * WORD_LANES, (j + 1) * WORD_LANES)
             nc.vector.quantize_mx(
                 out=z_codes[r][:, lanes, :].rearrange("p g b -> p (g b)").bitcast(FP8X4),
                 scales=z_scales[r][:, lanes, :].rearrange("p g b -> p (g b)"),
-                in_=z_grouped[r][:, lanes, :, :].rearrange("p g b t -> p (g b t)"),
+                in_=z_grouped[:].rearrange("p g b t -> p (g b t)"),
             )
 
         def layer1(r, g):
             sorted_sums = []
             for c in range(HID_PASSES):
                 hid_cols = slice(c * K_PASS, (c + 1) * K_PASS)
-                acc1 = psum.tile([P, K_PASS], F32, tag="acc1", bufs=2)
+                acc1 = psum.tile([P, K_PASS], F32, tag="bank")
                 nc.tensor.matmul_mx(
                     out=acc1[:],
                     lhsT=z_codes[r][:, g, :].bitcast(FP8X4),
@@ -171,10 +170,10 @@ def tile_blockresmlp_mixerblock_pa_e_kernel(
                 sorted_sums.append(v)
             return sorted_sums
 
-        def elu_and_quantise(r, g, sorted_sums):
+        def elu(sorted_sums):
             h_grouped = work.tile([P, HID_PASSES, P, PACK], BF16, tag="h_grouped", bufs=2, align_bytes=64)
             for c in range(HID_PASSES):
-                vt = psum.tile([P, PACK, P], F32, tag="transposed", bufs=4)
+                vt = psum.tile([P, PACK, P], F32, tag="bank")
                 for t in range(PACK):
                     nc.tensor.transpose(vt[:, t, :], sorted_sums[c][:, t, :], ident[:])
                 v_by_word = vt[:].rearrange("p t b -> p b t")
@@ -189,61 +188,66 @@ def tile_blockresmlp_mixerblock_pa_e_kernel(
                     op0=ALU.mult,
                     op1=ALU.max,
                 )
+            return h_grouped
+
+        def quantise_h(r, g, h_grouped):
             nc.vector.quantize_mx(
                 out=h_codes[r][:, g, :, :].rearrange("p c b -> p (c b)").bitcast(FP8X4),
                 scales=h_scales[r][:, g, :, :].rearrange("p c b -> p (c b)"),
                 in_=h_grouped[:].rearrange("p c b t -> p (c b t)"),
             )
 
-        def layer2(r, group):
-            for f in range(FEAT_CHUNKS):
-                feats = slice(f * FEAT_CHUNK, (f + 1) * FEAT_CHUNK)
-                acc2 = psum.tile([P, LANE_GROUP, FEAT_CHUNK], F32, tag="acc2", bufs=2)
-                for i in range(LANE_GROUP):
-                    g = group * LANE_GROUP + i
-                    for c in range(HID_PASSES):
-                        k_group = g * HID_PASSES + c
-                        nc.tensor.matmul_mx(
-                            out=acc2[:, i, :],
-                            lhsT=h_codes[r][:, g, c, :].bitcast(FP8X4),
-                            lhsT_scale=h_scales[r][:, g, c, :],
-                            rhs=w2_codes[:, k_group, feats].bitcast(FP8X4),
-                            rhs_scale=w2_planes[4 * (k_group % 4) : P, k_group // 4, feats],
-                            start=(c == 0),
-                            stop=(c == HID_PASSES - 1),
-                        )
-                lanes = slice(group * LANE_GROUP, (group + 1) * LANE_GROUP)
-                nc.vector.tensor_tensor(
-                    out=result[r][:, feats, lanes],
-                    in0=acc2[:].rearrange("b g d -> b d g"),
-                    in1=result[r][:, feats, lanes],
-                    op=ALU.add,
-                )
-                if group == GROUPS - 1:
-                    nc.sync.dma_start(
-                        out=out[r * P : (r + 1) * P, f * FEAT_CHUNK * LANES : (f + 1) * FEAT_CHUNK * LANES],
-                        in_=result[r][:, feats, :].rearrange("b d g -> b (d g)"),
+        def layer2(r, group, f):
+            feats = slice(f * FEAT_CHUNK, (f + 1) * FEAT_CHUNK)
+            acc2 = psum.tile([P, LANE_GROUP, FEAT_CHUNK], F32, tag="bank")
+            for m in range(LANE_GROUP):
+                g = group * LANE_GROUP + m
+                for c in range(HID_PASSES):
+                    k_group = g * HID_PASSES + c
+                    nc.tensor.matmul_mx(
+                        out=acc2[:, m, :],
+                        lhsT=h_codes[r][:, g, c, :].bitcast(FP8X4),
+                        lhsT_scale=h_scales[r][:, g, c, :],
+                        rhs=w2_codes[:, k_group, feats].bitcast(FP8X4),
+                        rhs_scale=w2_planes[4 * (k_group % 4) : P, k_group // 4, feats],
+                        start=(c == 0),
+                        stop=(c == HID_PASSES - 1),
                     )
+            lanes = slice(group * LANE_GROUP, (group + 1) * LANE_GROUP)
+            nc.vector.tensor_tensor(
+                out=result[r][:, feats, lanes],
+                in0=acc2[:].rearrange("b g d -> b d g"),
+                in1=result[r][:, feats, lanes],
+                op=ALU.add,
+            )
+            if group == GROUPS - 1:
+                nc.sync.dma_start(
+                    out=out[r * P : (r + 1) * P, f * FEAT_CHUNK * LANES : (f + 1) * FEAT_CHUNK * LANES],
+                    in_=result[r][:, feats, :].rearrange("b d g -> b (d g)"),
+                )
 
-        for pair in range(LANES // WORD_LANES):
-            transpose_z(0, pair)
-            if pair % 2 == 1:
-                quantise_z(0, pair // 2)
         for r in range(ROW_TILES):
             residual_plus_bias(r)
 
         units = [(r, g) for r in range(ROW_TILES) for g in range(LANES)]
-        ahead = layer1(*units[0])
-        for i, (r, g) in enumerate(units):
-            sums = ahead
-            if r + 1 < ROW_TILES and g % 2 == 0:
-                transpose_z(r + 1, g // 2)
-                if g % 4 == 2:
-                    quantise_z(r + 1, g // 4)
+        chunks = [(r, group, f) for r in range(ROW_TILES) for group in range(GROUPS) for f in range(FEAT_CHUNKS)]
+        pairs = ROW_TILES * PAIRS_PER_TILE
+
+        quantise_z(0, transpose_z(0))
+        z_waiting = transpose_z(1)
+        sums_ahead = layer1(*units[0])
+        h_waiting = None
+        for i in range(len(chunks) + L2_LAG):
+            sums = sums_ahead
             if i + 1 < len(units):
-                ahead = layer1(*units[i + 1])
-            elu_and_quantise(r, g, sums)
-            if i > 0 and i % LANE_GROUP == 0:
-                done = i // LANE_GROUP - 1
-                layer2(done // GROUPS, done % GROUPS)
-        layer2(ROW_TILES - 1, GROUPS - 1)
+                sums_ahead = layer1(*units[i + 1])
+            if 1 <= i <= len(units):
+                quantise_h(units[i - 1][0], units[i - 1][1], h_waiting)
+            if i % 2 == 0 and i // 2 + 1 < pairs:
+                quantise_z(i // 2 + 1, z_waiting)
+            if i < len(units):
+                h_waiting = elu(sums)
+            if i % 2 == 1 and i // 2 + 2 < pairs:
+                z_waiting = transpose_z(i // 2 + 2)
+            if i >= L2_LAG:
+                layer2(*chunks[i - L2_LAG])

@@ -15,6 +15,7 @@ ACT = mybir.ActivationFunctionType
 P = 128
 PACK = 4
 K_PASS = P * PACK
+BANK = 512
 LANES = 8
 BLOCK = 512
 HID = 1024
@@ -26,11 +27,13 @@ GROUPS = LANES // LANE_GROUP
 FEAT_CHUNK = P
 FEAT_CHUNKS = BLOCK // FEAT_CHUNK
 WORD_LANES = 2
-PAIRS_PER_TILE = LANES // WORD_LANES
-K_STEP = PACK * PAIRS_PER_TILE
+PAIRS = LANES // WORD_LANES
+K_STEP = PACK * PAIRS
 QUADRANTS = 4
-PSUM_BANKS = 8
-L2_LAG = 7
+RES_FEATS = BANK // LANES
+RES_CHUNKS = BLOCK // RES_FEATS
+COLS_TOGETHER = 4
+V_RELU = (3,)
 
 FLOPS = 2 * LANES * ROWS * (BLOCK * HID + HID * BLOCK)
 
@@ -42,54 +45,52 @@ def tile_blockresmlp_mixerblock_pa_e_kernel(
     with ExitStack() as ctx:
         keep = ctx.enter_context(tc.tile_pool(name="keep", bufs=1))
         work = ctx.enter_context(tc.tile_pool(name="work", bufs=2))
-        psum = ctx.enter_context(tc.psum_pool(name="psum", bufs=PSUM_BANKS))
+        psum = ctx.enter_context(tc.psum_pool(name="psum", bufs=2))
         ctx.enter_context(tc.manual_schedule())
 
         ident = keep.tile([P, P], F32)
-        make_identity(nc, ident[:])
+        ones = keep.tile([P, P], BF16)
         warm = keep.tile([P, 1], F32)
-        nc.vector.memset(warm[:], 0.0)
-        nc.scalar.activation(out=warm[:], in_=warm[:], func=ACT.Exp)
-
+        b1_rows = keep.tile([P, BLOCK], BF16, align_bytes=64)
+        b1_cols = keep.tile([P, LANES * HID_PASSES, PACK], F32)
+        b2_row = keep.tile([P, LANES, BLOCK], BF16)
         y_sb = [keep.tile([P, BLOCK * LANES], BF16, name="y%d" % r) for r in range(ROW_TILES)]
-        w1_codes = keep.tile([P, LANES, HID], U32, align_bytes=64)
+        w1_raw = keep.tile([P, LANES, HID], U32, align_bytes=64)
+        w1_codes = keep.tile([P, LANES, HID_PASSES, PACK, P], U32, align_bytes=64)
+        w1_raw_planes = keep.tile([P, GROUPS, HID], U8, align_bytes=64)
+        w1_planes = keep.tile([P, GROUPS, HID_PASSES, PACK, P], U8, align_bytes=64)
         w2_codes = keep.tile([P, LANES * HID_PASSES, BLOCK], U32, align_bytes=64)
-        w1_planes = keep.tile([P, GROUPS, HID], U8, align_bytes=64)
         w2_planes = keep.tile([P, GROUPS * HID_PASSES, BLOCK], U8, align_bytes=64)
-        b1_all = keep.tile([P, LANES, HID], BF16)
-        b2_all = keep.tile([P, LANES, BLOCK], BF16)
         result = [keep.tile([P, BLOCK, LANES], F32, name="result%d" % r) for r in range(ROW_TILES)]
-        z_codes = [keep.tile([P, LANES, P], U32, name="z_codes%d" % r, align_bytes=64) for r in range(ROW_TILES)]
-        z_scales = [keep.tile([P, LANES, P], U8, name="z_scales%d" % r, align_bytes=64) for r in range(ROW_TILES)]
-        h_codes = [
-            keep.tile([P, LANES, HID_PASSES, P], U32, name="h_codes%d" % r, align_bytes=64)
-            for r in range(ROW_TILES)
-        ]
-        h_scales = [
-            keep.tile([P, LANES, HID_PASSES, P], U8, name="h_scales%d" % r, align_bytes=64)
-            for r in range(ROW_TILES)
-        ]
+        z_codes = keep.tile([P, LANES, ROWS], U32, align_bytes=64)
+        z_scales = keep.tile([P, LANES, ROWS], U8, align_bytes=64)
+        h_codes = keep.tile([P, LANES * HID_PASSES, ROWS], U32, align_bytes=64)
+        h_scales = keep.tile([P, LANES * HID_PASSES, ROWS], U8, align_bytes=64)
 
-        nc.vector.memset(w1_planes[:].bitcast(I32), 0)
+        nc.vector.memset(warm[:], 0.0)
+        nc.vector.memset(w1_raw_planes[:].bitcast(I32), 0)
         nc.vector.memset(w2_planes[:].bitcast(I32), 0)
+        nc.vector.memset(ones[:], 1.0)
+        nc.scalar.activation(out=warm[:], in_=warm[:], func=ACT.Exp)
+        nc.gpsimd.memset(b1_rows[:].bitcast(I32), 0)
+        make_identity(nc, ident[:])
+        nc.gpsimd.memset(b2_row[:].bitcast(I32), 0)
 
         def load_y(r):
             nc.sync.dma_start(out=y_sb[r][:], in_=y_lanes[r * P : (r + 1) * P, :])
 
-        def load_planes(planes, scales, tiles):
-            for j in range(tiles):
-                for quad in range(QUADRANTS):
-                    nc.sync.dma_start(
-                        out=planes[32 * quad : 32 * quad + 16, j, :].bitcast(I32),
-                        in_=scales[4 * j : 4 * j + 4, 4 * quad : 4 * quad + 4, :].bitcast(I32),
-                    )
+        def load_planes(planes, scales, j):
+            for quad in range(QUADRANTS):
+                nc.sync.dma_start(
+                    out=planes[32 * quad : 32 * quad + 16, j, :].bitcast(I32),
+                    in_=scales[4 * j : 4 * j + 4, 4 * quad : 4 * quad + 4, :].bitcast(I32),
+                )
 
-        def load_layer1(g):
+        def load_w1(g):
             nc.sync.dma_start(
-                out=w1_codes[:, g, :].bitcast(I32),
+                out=w1_raw[:, g, :].bitcast(I32),
                 in_=w1_words[g].rearrange("p n t -> p (n t)").bitcast(I32),
             )
-            nc.sync.dma_start(out=b1_all[:, g, :], in_=b1[g].rearrange("o n -> (o n)").partition_broadcast(P))
 
         def load_w2(g):
             passes = slice(g * HID_PASSES, (g + 1) * HID_PASSES)
@@ -98,121 +99,174 @@ def tile_blockresmlp_mixerblock_pa_e_kernel(
                 in_=w2_words[passes].rearrange("c p n t -> p c (n t)").bitcast(I32),
             )
 
-        load_y(0)
-        load_planes(w1_planes, w1_scales, GROUPS)
-        for g in range(LANE_GROUP):
-            load_layer1(g)
-        nc.sync.dma_start(
-            out=b2_all[:].rearrange("p g n -> p (g n)"),
-            in_=b2.rearrange("g o n -> (g o n)").partition_broadcast(P),
+        nc.scalar.dma_start(
+            out=b1_rows[0 : LANES * HID_PASSES, :], in_=b1.rearrange("g o (c n) -> (g o c) n", c=HID_PASSES)
         )
+        nc.scalar.dma_start(
+            out=b2_row[0:1, :, :].rearrange("p g n -> p (g n)"), in_=b2.rearrange("g o n -> o (g n)")
+        )
+        load_y(0)
+        load_planes(w1_raw_planes, w1_scales, 0)
+        load_w1(0)
         load_y(1)
-        for g in range(LANE_GROUP, LANES):
-            load_layer1(g)
-        load_planes(w2_planes, w2_scales, GROUPS * HID_PASSES)
+        load_w1(1)
+        load_planes(w1_raw_planes, w1_scales, 1)
+        for g in range(2, LANES):
+            load_w1(g)
+        for j in range(GROUPS * HID_PASSES):
+            load_planes(w2_planes, w2_scales, j)
         for g in range(LANES):
             load_w2(g)
 
-        def residual_plus_bias(r):
-            for f in range(FEAT_CHUNKS):
-                feats = slice(f * FEAT_CHUNK, (f + 1) * FEAT_CHUNK)
-                nc.gpsimd.tensor_tensor(
-                    out=result[r][:, feats, :],
-                    in0=y_sb[r][:].rearrange("b (d g) -> b d g", g=LANES)[:, feats, :],
-                    in1=b2_all[:, :, feats].rearrange("b g d -> b d g"),
-                    op=ALU.add,
+        def bias_columns():
+            words = b1_rows[:].bitcast(F32)
+            bank = psum.tile([P, 2, P], F32, tag="small", bufs=2)
+            for u in range(2):
+                nc.tensor.transpose(bank[:, u, :], words[:, u : BLOCK // 2 : 2], ident[:])
+            nc.vector.tensor_copy(
+                out=b1_cols[:].rearrange("p r (u e) -> p u r e", e=2),
+                in_=bank[:].bitcast(BF16).rearrange("p u (r e) -> p u r e", e=2)[:, :, 0 : LANES * HID_PASSES, :],
+            )
+
+        def sort_planes(j):
+            nc.vector.tensor_copy(
+                out=w1_planes[:, j, :, :, :].rearrange("p c t m -> p c m t"),
+                in_=w1_raw_planes[:, j, :].rearrange("p (c m t) -> p c m t", c=HID_PASSES, t=PACK),
+            )
+
+        def sort_codes(g):
+            for c in range(HID_PASSES):
+                nc.vector.tensor_copy(
+                    out=w1_codes[:, g, c, :, :].bitcast(I32).rearrange("p t (a i) -> p a t i", i=COLS_TOGETHER),
+                    in_=w1_raw[:, g, c * K_PASS : (c + 1) * K_PASS]
+                    .bitcast(I32)
+                    .rearrange("p (a i t) -> p a t i", i=COLS_TOGETHER, t=PACK),
                 )
 
-        def transpose_z(pair):
-            r, j = divmod(pair, PAIRS_PER_TILE)
+        def residual_plus_bias(r, q):
+            feats = slice(q * RES_FEATS, (q + 1) * RES_FEATS)
+            bank = psum.tile([P, RES_FEATS, LANES], F32, tag="small", bufs=2)
+            nc.tensor.matmul(
+                bank[:], lhsT=ones[:], rhs=b2_row[:, :, feats].rearrange("p g d -> p d g"), start=True, stop=True
+            )
+            nc.vector.tensor_tensor(
+                out=result[r][:, feats, :],
+                in0=bank[:],
+                in1=y_sb[r][:].rearrange("b (d g) -> b d g", g=LANES)[:, feats, :],
+                op=ALU.add,
+            )
+
+        def transpose_z(j, r, z_grouped, at):
             y_words = y_sb[r][:].bitcast(F32)
-            zt = psum.tile([P, PACK, P], F32, tag="bank")
+            zt = psum.tile([P, PACK, P], F32, tag="small", bufs=2)
             for t in range(PACK):
-                first = t * PAIRS_PER_TILE + j
-                nc.tensor.transpose(zt[:, t, :], y_words[:, first : BLOCK * PAIRS_PER_TILE : K_STEP], ident[:])
-            z_grouped = work.tile([P, WORD_LANES, P, PACK], BF16, tag="z_grouped", bufs=2, align_bytes=64)
+                first = t * PAIRS + j
+                nc.tensor.transpose(zt[:, t, :], y_words[:, first : BLOCK * PAIRS : K_STEP], ident[:])
             nc.scalar.copy(
-                out=z_grouped[:],
+                out=z_grouped[:, :, at : at + P, :],
                 in_=zt[:].bitcast(BF16).rearrange("p t (b e) -> p e b t", e=WORD_LANES),
             )
-            return z_grouped
 
-        def quantise_z(pair, z_grouped):
-            r, j = divmod(pair, PAIRS_PER_TILE)
+        def quantise_z(j, z_grouped):
             lanes = slice(j * WORD_LANES, (j + 1) * WORD_LANES)
             nc.vector.quantize_mx(
-                out=z_codes[r][:, lanes, :].rearrange("p g b -> p (g b)").bitcast(FP8X4),
-                scales=z_scales[r][:, lanes, :].rearrange("p g b -> p (g b)"),
+                out=z_codes[:, lanes, :].rearrange("p g b -> p (g b)").bitcast(FP8X4),
+                scales=z_scales[:, lanes, :].rearrange("p g b -> p (g b)"),
                 in_=z_grouped[:].rearrange("p g b t -> p (g b t)"),
             )
 
-        def layer1(r, g):
-            sorted_sums = []
-            for c in range(HID_PASSES):
-                hid_cols = slice(c * K_PASS, (c + 1) * K_PASS)
-                acc1 = psum.tile([P, K_PASS], F32, tag="bank")
+        def quantise_z_tile(j, r, z_grouped):
+            for e in range(WORD_LANES):
+                nc.vector.quantize_mx(
+                    out=z_codes[:, j * WORD_LANES + e, r * P : (r + 1) * P].bitcast(FP8X4),
+                    scales=z_scales[:, j * WORD_LANES + e, r * P : (r + 1) * P],
+                    in_=z_grouped[:, e, :, :].rearrange("p b t -> p (b t)"),
+                )
+
+        def layer1(step):
+            g, c, rows = step
+            width = rows.stop - rows.start
+            per_bank = BANK // width
+            plane = 4 * (g % LANE_GROUP)
+            sums = []
+            for t in range(PACK):
+                if t % per_bank == 0:
+                    acc1 = psum.tile([P, per_bank, width], F32, tag="acc1", bufs=4)
+                sums.append(acc1[:, t % per_bank, :])
                 nc.tensor.matmul_mx(
-                    out=acc1[:],
-                    lhsT=z_codes[r][:, g, :].bitcast(FP8X4),
-                    lhsT_scale=z_scales[r][:, g, :],
-                    rhs=w1_codes[:, g, hid_cols].bitcast(FP8X4),
-                    rhs_scale=w1_planes[4 * (g % LANE_GROUP) : P, g // LANE_GROUP, hid_cols],
+                    out=sums[t],
+                    lhsT=w1_codes[:, g, c, t, :].bitcast(FP8X4),
+                    lhsT_scale=w1_planes[plane:P, g // LANE_GROUP, c, t, :],
+                    rhs=z_codes[:, g, rows].bitcast(FP8X4),
+                    rhs_scale=z_scales[:, g, rows],
                     start=True,
                     stop=True,
                 )
-                v = work.tile([P, PACK, P], F32, tag="v", bufs=4)
-                nc.vector.tensor_tensor(
-                    out=v[:],
-                    in0=acc1[:].rearrange("b (p t) -> b t p", t=PACK),
-                    in1=b1_all[:, g, hid_cols].rearrange("b (p t) -> b t p", t=PACK),
-                    op=ALU.add,
-                )
-                sorted_sums.append(v)
-            return sorted_sums
+            return sums
 
-        def elu(sorted_sums):
-            h_grouped = work.tile([P, HID_PASSES, P, PACK], BF16, tag="h_grouped", bufs=2, align_bytes=64)
-            for c in range(HID_PASSES):
-                vt = psum.tile([P, PACK, P], F32, tag="bank")
-                for t in range(PACK):
-                    nc.tensor.transpose(vt[:, t, :], sorted_sums[c][:, t, :], ident[:])
-                v_by_word = vt[:].rearrange("p t b -> p b t")
-                gap = work.tile([P, P, PACK], F32, tag="gap", bufs=3)
-                nc.scalar.activation(out=gap[:], in_=v_by_word, func=ACT.Exp)
-                nc.scalar.activation(out=gap[:], in_=gap[:], func=ACT.Relu, scale=-1.0, bias=1.0)
-                nc.vector.scalar_tensor_tensor(
-                    out=h_grouped[:, c, :, :],
-                    in0=gap[:],
-                    scalar=-1.0,
-                    in1=v_by_word,
-                    op0=ALU.mult,
-                    op1=ALU.max,
+        def exp_and_relu(step, sums):
+            g, c, rows = step
+            width = rows.stop - rows.start
+            e = work.tile([P, PACK, width], F32, tag="e", bufs=3)
+            pos = work.tile([P, PACK, width], BF16, tag="pos", bufs=3)
+
+            def bias(t):
+                return b1_cols[:, g * HID_PASSES + c, t : t + 1]
+
+            on_vector = V_RELU if width == ROWS else ()
+            for t in on_vector:
+                nc.vector.tensor_scalar(
+                    out=pos[:, t, :], in0=sums[t], scalar1=bias(t), scalar2=0.0, op0=ALU.add, op1=ALU.max
                 )
+            for t in range(PACK):
+                nc.scalar.activation(out=e[:, t, :], in_=sums[t], func=ACT.Exp, bias=bias(t))
+                if t not in on_vector:
+                    nc.scalar.activation(out=pos[:, t, :], in_=sums[t], func=ACT.Relu, bias=bias(t))
+            return e, pos
+
+        def elu(step, parts):
+            g, c, rows = step
+            e, pos = parts
+            h_grouped = work.tile([P, rows.stop - rows.start, PACK], BF16, tag="h_grouped", bufs=3, align_bytes=64)
+            nc.vector.scalar_tensor_tensor(
+                out=h_grouped[:],
+                in0=e[:].rearrange("p t b -> p b t"),
+                scalar=-1.0,
+                in1=pos[:].rearrange("p t b -> p b t"),
+                op0=ALU.add,
+                op1=ALU.min,
+            )
             return h_grouped
 
-        def quantise_h(r, g, h_grouped):
+        def quantise_h(step, h_grouped):
+            g, c, rows = step
+            k_group = g * HID_PASSES + c
             nc.vector.quantize_mx(
-                out=h_codes[r][:, g, :, :].rearrange("p c b -> p (c b)").bitcast(FP8X4),
-                scales=h_scales[r][:, g, :, :].rearrange("p c b -> p (c b)"),
-                in_=h_grouped[:].rearrange("p c b t -> p (c b t)"),
+                out=h_codes[:, k_group, rows].bitcast(FP8X4),
+                scales=h_scales[:, k_group, rows],
+                in_=h_grouped[:].rearrange("p b t -> p (b t)"),
             )
 
-        def layer2(r, group, f):
+        def layer2(group, r, f):
             feats = slice(f * FEAT_CHUNK, (f + 1) * FEAT_CHUNK)
-            acc2 = psum.tile([P, LANE_GROUP, FEAT_CHUNK], F32, tag="bank")
+            rows = slice(r * P, (r + 1) * P)
+            acc2 = psum.tile([P, LANE_GROUP, FEAT_CHUNK], F32, tag="acc2", bufs=2)
             for m in range(LANE_GROUP):
-                g = group * LANE_GROUP + m
                 for c in range(HID_PASSES):
-                    k_group = g * HID_PASSES + c
+                    k_group = (group * LANE_GROUP + m) * HID_PASSES + c
                     nc.tensor.matmul_mx(
                         out=acc2[:, m, :],
-                        lhsT=h_codes[r][:, g, c, :].bitcast(FP8X4),
-                        lhsT_scale=h_scales[r][:, g, c, :],
+                        lhsT=h_codes[:, k_group, rows].bitcast(FP8X4),
+                        lhsT_scale=h_scales[:, k_group, rows],
                         rhs=w2_codes[:, k_group, feats].bitcast(FP8X4),
                         rhs_scale=w2_planes[4 * (k_group % 4) : P, k_group // 4, feats],
                         start=(c == 0),
                         stop=(c == HID_PASSES - 1),
                     )
+            return acc2
+
+        def add_layer2(group, r, f, acc2):
+            feats = slice(f * FEAT_CHUNK, (f + 1) * FEAT_CHUNK)
             lanes = slice(group * LANE_GROUP, (group + 1) * LANE_GROUP)
             nc.vector.tensor_tensor(
                 out=result[r][:, feats, lanes],
@@ -226,28 +280,76 @@ def tile_blockresmlp_mixerblock_pa_e_kernel(
                     in_=result[r][:, feats, :].rearrange("b d g -> b (d g)"),
                 )
 
-        for r in range(ROW_TILES):
-            residual_plus_bias(r)
+        both = slice(0, ROWS)
+        tiles = [slice(r * P, (r + 1) * P) for r in range(ROW_TILES)]
+        lanes_rows = [(0, tiles[0]), (0, tiles[1])]
+        lanes_rows += [(g, both) for g in range(1, LANES - 2)]
+        lanes_rows += [(g, tiles[r]) for r in range(ROW_TILES) for g in (LANES - 2, LANES - 1)]
+        steps = [(g, c, rows) for g, rows in lanes_rows for c in range(HID_PASSES)]
+        first = [min(i for i, s in enumerate(steps) if s[0] == g) for g in range(LANES)]
 
-        units = [(r, g) for r in range(ROW_TILES) for g in range(LANES)]
-        chunks = [(r, group, f) for r in range(ROW_TILES) for group in range(GROUPS) for f in range(FEAT_CHUNKS)]
-        pairs = ROW_TILES * PAIRS_PER_TILE
+        def last(group, r):
+            return max(
+                i
+                for i, s in enumerate(steps)
+                if s[0] // LANE_GROUP == group and s[2].start <= r * P < s[2].stop
+            )
 
-        quantise_z(0, transpose_z(0))
-        z_waiting = transpose_z(1)
-        sums_ahead = layer1(*units[0])
-        h_waiting = None
-        for i in range(len(chunks) + L2_LAG):
+        chunks = [(group, r, f) for group in range(GROUPS) for r in range(ROW_TILES) for f in range(FEAT_CHUNKS)]
+        residuals = [(r, q) for r in range(ROW_TILES) for q in range(RES_CHUNKS)]
+
+        def new_z(width):
+            return work.tile([P, WORD_LANES, width, PACK], BF16, tag="z_grouped", bufs=2, align_bytes=64, name="z_grouped")
+
+        bias_columns()
+        sort_planes(0)
+        z_first = new_z(P)
+        transpose_z(0, 0, z_first, 0)
+        residual_plus_bias(*residuals.pop(0))
+        residual_plus_bias(*residuals.pop(0))
+        quantise_z_tile(0, 0, z_first)
+        sort_codes(0)
+        residual_plus_bias(*residuals.pop(0))
+        sums_ahead = layer1(steps[0])
+        parts_before = None
+        z_waiting = None
+        z_tile_one = None
+        for i in range(len(steps) + 1):
             sums = sums_ahead
-            if i + 1 < len(units):
-                sums_ahead = layer1(*units[i + 1])
-            if 1 <= i <= len(units):
-                quantise_h(units[i - 1][0], units[i - 1][1], h_waiting)
-            if i % 2 == 0 and i // 2 + 1 < pairs:
-                quantise_z(i // 2 + 1, z_waiting)
-            if i < len(units):
-                h_waiting = elu(sums)
-            if i % 2 == 1 and i // 2 + 2 < pairs:
-                z_waiting = transpose_z(i // 2 + 2)
-            if i >= L2_LAG:
-                layer2(*chunks[i - L2_LAG])
+            if i == 0:
+                z_tile_one = new_z(P)
+            if i + 1 < len(steps):
+                sums_ahead = layer1(steps[i + 1])
+            ready = [ch for ch in chunks if last(ch[0], ch[1]) + 2 <= i]
+            chunk = ready[0] if ready else None
+            if chunk:
+                chunks.remove(chunk)
+                acc2 = layer2(*chunk)
+            parts = exp_and_relu(steps[i], sums) if i < len(steps) else None
+            h_grouped = elu(steps[i - 1], parts_before) if i >= 1 else None
+            parts_before = parts
+            if i == 0:
+                transpose_z(0, 1, z_tile_one, 0)
+                quantise_z_tile(0, 1, z_tile_one)
+            for j in range(1, PAIRS):
+                start = first[j * WORD_LANES] - 4
+                if i == start:
+                    z_waiting = new_z(ROWS)
+                    transpose_z(j, 0, z_waiting, 0)
+                if i == start + 1:
+                    transpose_z(j, 1, z_waiting, P)
+                if i == start + 2:
+                    quantise_z(j, z_waiting)
+            for g in range(1, LANES):
+                if i == first[g] - 3:
+                    sort_codes(g)
+            if i == first[LANE_GROUP] - 4:
+                sort_planes(1)
+            if chunk:
+                add_layer2(*chunk, acc2)
+            if residuals:
+                residual_plus_bias(*residuals.pop(0))
+            if i >= 1:
+                quantise_h(steps[i - 1], h_grouped)
+        for chunk in chunks:
+            add_layer2(*chunk, layer2(*chunk))

@@ -32,8 +32,8 @@ K_STEP = PACK * PAIRS
 QUADRANTS = 4
 RES_FEATS = BANK // LANES
 RES_CHUNKS = BLOCK // RES_FEATS
+SCALAR_RESIDUALS = 2
 COLS_TOGETHER = 4
-V_RELU = (3,)
 
 FLOPS = 2 * LANES * ROWS * (BLOCK * HID + HID * BLOCK)
 
@@ -49,6 +49,7 @@ def tile_blockresmlp_mixerblock_pa_e_kernel(
         ctx.enter_context(tc.manual_schedule())
 
         ident = keep.tile([P, P], F32)
+        ident_bf16 = keep.tile([P, P], BF16)
         ones = keep.tile([P, P], BF16)
         warm = keep.tile([P, 1], F32)
         b1_rows = keep.tile([P, BLOCK], BF16, align_bytes=64)
@@ -68,13 +69,14 @@ def tile_blockresmlp_mixerblock_pa_e_kernel(
         h_scales = keep.tile([P, LANES * HID_PASSES, ROWS], U8, align_bytes=64)
 
         nc.vector.memset(warm[:], 0.0)
+        nc.vector.memset(b2_row[:].bitcast(I32), 0)
         nc.vector.memset(w1_raw_planes[:].bitcast(I32), 0)
         nc.vector.memset(w2_planes[:].bitcast(I32), 0)
         nc.vector.memset(ones[:], 1.0)
         nc.scalar.activation(out=warm[:], in_=warm[:], func=ACT.Exp)
         nc.gpsimd.memset(b1_rows[:].bitcast(I32), 0)
         make_identity(nc, ident[:])
-        nc.gpsimd.memset(b2_row[:].bitcast(I32), 0)
+        nc.vector.tensor_copy(out=ident_bf16[:], in_=ident[:])
 
         def load_y(r):
             nc.sync.dma_start(out=y_sb[r][:], in_=y_lanes[r * P : (r + 1) * P, :])
@@ -99,13 +101,13 @@ def tile_blockresmlp_mixerblock_pa_e_kernel(
                 in_=w2_words[passes].rearrange("c p n t -> p c (n t)").bitcast(I32),
             )
 
-        nc.scalar.dma_start(
+        nc.sync.dma_start(
             out=b1_rows[0 : LANES * HID_PASSES, :], in_=b1.rearrange("g o (c n) -> (g o c) n", c=HID_PASSES)
         )
-        nc.scalar.dma_start(
+        load_y(0)
+        nc.sync.dma_start(
             out=b2_row[0:1, :, :].rearrange("p g n -> p (g n)"), in_=b2.rearrange("g o n -> o (g n)")
         )
-        load_y(0)
         load_planes(w1_raw_planes, w1_scales, 0)
         load_w1(0)
         load_y(1)
@@ -143,12 +145,16 @@ def tile_blockresmlp_mixerblock_pa_e_kernel(
                     .rearrange("p (a i t) -> p a t i", i=COLS_TOGETHER, t=PACK),
                 )
 
-        def residual_plus_bias(r, q):
+        def spread_b2(q):
             feats = slice(q * RES_FEATS, (q + 1) * RES_FEATS)
             bank = psum.tile([P, RES_FEATS, LANES], F32, tag="small", bufs=2)
             nc.tensor.matmul(
                 bank[:], lhsT=ones[:], rhs=b2_row[:, :, feats].rearrange("p g d -> p d g"), start=True, stop=True
             )
+            return bank
+
+        def residual_plus_bias(r, q, bank):
+            feats = slice(q * RES_FEATS, (q + 1) * RES_FEATS)
             nc.vector.tensor_tensor(
                 out=result[r][:, feats, :],
                 in0=bank[:],
@@ -156,16 +162,35 @@ def tile_blockresmlp_mixerblock_pa_e_kernel(
                 op=ALU.add,
             )
 
-        def transpose_z(j, r, z_grouped, at):
+        def residual_by_matmul(r, q):
+            feats = slice(q * RES_FEATS, (q + 1) * RES_FEATS)
+            bank = psum.tile([P, RES_FEATS, LANES], F32, tag="acc2", bufs=2)
+            nc.tensor.matmul(
+                bank[:],
+                lhsT=ident_bf16[:],
+                rhs=y_sb[r][:].rearrange("b (d g) -> b d g", g=LANES)[:, feats, :],
+                start=True,
+                stop=False,
+            )
+            nc.tensor.matmul(
+                bank[:], lhsT=ones[:], rhs=b2_row[:, :, feats].rearrange("p g d -> p d g"), start=False, stop=True
+            )
+            nc.scalar.copy(out=result[r][:, feats, :], in_=bank[:])
+
+        def transpose_z(j, r):
             y_words = y_sb[r][:].bitcast(F32)
             zt = psum.tile([P, PACK, P], F32, tag="small", bufs=2)
             for t in range(PACK):
                 first = t * PAIRS + j
                 nc.tensor.transpose(zt[:, t, :], y_words[:, first : BLOCK * PAIRS : K_STEP], ident[:])
-            nc.scalar.copy(
-                out=z_grouped[:, :, at : at + P, :],
-                in_=zt[:].bitcast(BF16).rearrange("p t (b e) -> p e b t", e=WORD_LANES),
-            )
+            return zt
+
+        def copy_z(zt, z_grouped, at):
+            for e in range(WORD_LANES):
+                nc.scalar.copy(
+                    out=z_grouped[:, e, at : at + P, :],
+                    in_=zt[:].bitcast(BF16).rearrange("p t (b e) -> p e b t", e=WORD_LANES)[:, e, :, :],
+                )
 
         def quantise_z(j, z_grouped):
             lanes = slice(j * WORD_LANES, (j + 1) * WORD_LANES)
@@ -213,15 +238,9 @@ def tile_blockresmlp_mixerblock_pa_e_kernel(
             def bias(t):
                 return b1_cols[:, g * HID_PASSES + c, t : t + 1]
 
-            on_vector = V_RELU if width == ROWS else ()
-            for t in on_vector:
-                nc.vector.tensor_scalar(
-                    out=pos[:, t, :], in0=sums[t], scalar1=bias(t), scalar2=0.0, op0=ALU.add, op1=ALU.max
-                )
             for t in range(PACK):
                 nc.scalar.activation(out=e[:, t, :], in_=sums[t], func=ACT.Exp, bias=bias(t))
-                if t not in on_vector:
-                    nc.scalar.activation(out=pos[:, t, :], in_=sums[t], func=ACT.Relu, bias=bias(t))
+                nc.scalar.activation(out=pos[:, t, :], in_=sums[t], func=ACT.Relu, bias=bias(t))
             return e, pos
 
         def elu(step, parts):
@@ -304,13 +323,14 @@ def tile_blockresmlp_mixerblock_pa_e_kernel(
         bias_columns()
         sort_planes(0)
         z_first = new_z(P)
-        transpose_z(0, 0, z_first, 0)
-        residual_plus_bias(*residuals.pop(0))
-        residual_plus_bias(*residuals.pop(0))
-        quantise_z_tile(0, 0, z_first)
+        copy_z(transpose_z(0, 0), z_first, 0)
         sort_codes(0)
-        residual_plus_bias(*residuals.pop(0))
+        for q in range(SCALAR_RESIDUALS):
+            residual_by_matmul(*residuals.pop(0))
+        quantise_z_tile(0, 0, z_first)
         sums_ahead = layer1(steps[0])
+        zt = transpose_z(0, 1)
+        b2_ahead = spread_b2(residuals[0][1])
         parts_before = None
         z_waiting = None
         z_tile_one = None
@@ -329,15 +349,15 @@ def tile_blockresmlp_mixerblock_pa_e_kernel(
             h_grouped = elu(steps[i - 1], parts_before) if i >= 1 else None
             parts_before = parts
             if i == 0:
-                transpose_z(0, 1, z_tile_one, 0)
+                copy_z(zt, z_tile_one, 0)
                 quantise_z_tile(0, 1, z_tile_one)
             for j in range(1, PAIRS):
                 start = first[j * WORD_LANES] - 4
                 if i == start:
                     z_waiting = new_z(ROWS)
-                    transpose_z(j, 0, z_waiting, 0)
+                    copy_z(transpose_z(j, 0), z_waiting, 0)
                 if i == start + 1:
-                    transpose_z(j, 1, z_waiting, P)
+                    copy_z(transpose_z(j, 1), z_waiting, P)
                 if i == start + 2:
                     quantise_z(j, z_waiting)
             for g in range(1, LANES):
@@ -348,7 +368,9 @@ def tile_blockresmlp_mixerblock_pa_e_kernel(
             if chunk:
                 add_layer2(*chunk, acc2)
             if residuals:
-                residual_plus_bias(*residuals.pop(0))
+                residual_plus_bias(*residuals.pop(0), b2_ahead)
+                if residuals:
+                    b2_ahead = spread_b2(residuals[0][1])
             if i >= 1:
                 quantise_h(steps[i - 1], h_grouped)
         for chunk in chunks:

@@ -32,7 +32,8 @@ K_STEP = PACK * PAIRS
 QUADRANTS = 4
 RES_FEATS = BANK // LANES
 RES_CHUNKS = BLOCK // RES_FEATS
-SCALAR_RESIDUALS = 2
+HEAD_RESIDUALS = 2
+STEP_RESIDUALS = 7
 COLS_TOGETHER = 4
 
 FLOPS = 2 * LANES * ROWS * (BLOCK * HID + HID * BLOCK)
@@ -325,11 +326,12 @@ def tile_blockresmlp_mixerblock_pa_e_kernel(
         z_first = new_z(P)
         copy_z(transpose_z(0, 0), z_first, 0)
         sort_codes(0)
-        for q in range(SCALAR_RESIDUALS):
+        for q in range(HEAD_RESIDUALS):
             residual_by_matmul(*residuals.pop(0))
         quantise_z_tile(0, 0, z_first)
         sums_ahead = layer1(steps[0])
         zt = transpose_z(0, 1)
+        by_scalar = [residuals.pop(0) for q in range(STEP_RESIDUALS)]
         b2_ahead = spread_b2(residuals[0][1])
         parts_before = None
         z_waiting = None
@@ -351,6 +353,8 @@ def tile_blockresmlp_mixerblock_pa_e_kernel(
             if i == 0:
                 copy_z(zt, z_tile_one, 0)
                 quantise_z_tile(0, 1, z_tile_one)
+            if by_scalar:
+                residual_by_matmul(*by_scalar.pop(0))
             for j in range(1, PAIRS):
                 start = first[j * WORD_LANES] - 4
                 if i == start:

@@ -55,7 +55,8 @@ def tile_blockresmlp_mixerblock_pa_e_kernel(
         warm = keep.tile([P, 1], F32)
         b1_rows = keep.tile([P, BLOCK], BF16, align_bytes=64)
         b1_cols = keep.tile([P, LANES * HID_PASSES, PACK], F32)
-        b2_row = keep.tile([P, LANES, BLOCK], BF16)
+        b2_raw = keep.tile([P, LANES, BLOCK], BF16)
+        b2_row = keep.tile([P, BLOCK, LANES], BF16)
         y_sb = [keep.tile([P, BLOCK * LANES], BF16, name="y%d" % r) for r in range(ROW_TILES)]
         w1_raw = keep.tile([P, LANES, HID], U32, align_bytes=64)
         w1_codes = keep.tile([P, LANES, HID_PASSES, PACK, P], U32, align_bytes=64)
@@ -70,8 +71,8 @@ def tile_blockresmlp_mixerblock_pa_e_kernel(
         h_scales = keep.tile([P, LANES * HID_PASSES, ROWS], U8, align_bytes=64)
 
         nc.vector.memset(warm[:], 0.0)
-        nc.vector.memset(b2_row[:].bitcast(I32), 0)
         nc.vector.memset(w1_raw_planes[:].bitcast(I32), 0)
+        nc.vector.memset(b2_row[:].bitcast(I32), 0)
         nc.vector.memset(w2_planes[:].bitcast(I32), 0)
         nc.vector.memset(ones[:], 1.0)
         nc.scalar.activation(out=warm[:], in_=warm[:], func=ACT.Exp)
@@ -89,10 +90,10 @@ def tile_blockresmlp_mixerblock_pa_e_kernel(
                     in_=scales[4 * j : 4 * j + 4, 4 * quad : 4 * quad + 4, :].bitcast(I32),
                 )
 
-        def load_w1(g):
+        def load_w1(g, columns=slice(0, HID)):
             nc.sync.dma_start(
-                out=w1_raw[:, g, :].bitcast(I32),
-                in_=w1_words[g].rearrange("p n t -> p (n t)").bitcast(I32),
+                out=w1_raw[:, g, columns].bitcast(I32),
+                in_=w1_words[g][:, columns, :].rearrange("p n t -> p (n t)").bitcast(I32),
             )
 
         def load_w2(g):
@@ -102,15 +103,16 @@ def tile_blockresmlp_mixerblock_pa_e_kernel(
                 in_=w2_words[passes].rearrange("c p n t -> p c (n t)").bitcast(I32),
             )
 
+        nc.scalar.dma_start(
+            out=b2_raw[0:1, :, :].rearrange("p g n -> p (g n)"), in_=b2.rearrange("g o n -> o (g n)")
+        )
+        load_y(0)
+        load_planes(w1_raw_planes, w1_scales, 0)
         nc.sync.dma_start(
             out=b1_rows[0 : LANES * HID_PASSES, :], in_=b1.rearrange("g o (c n) -> (g o c) n", c=HID_PASSES)
         )
-        load_y(0)
-        nc.sync.dma_start(
-            out=b2_row[0:1, :, :].rearrange("p g n -> p (g n)"), in_=b2.rearrange("g o n -> o (g n)")
-        )
-        load_planes(w1_raw_planes, w1_scales, 0)
-        load_w1(0)
+        for c in range(HID_PASSES):
+            load_w1(0, slice(c * K_PASS, (c + 1) * K_PASS))
         load_y(1)
         load_w1(1)
         load_planes(w1_raw_planes, w1_scales, 1)
@@ -131,26 +133,31 @@ def tile_blockresmlp_mixerblock_pa_e_kernel(
                 in_=bank[:].bitcast(BF16).rearrange("p u (r e) -> p u r e", e=2)[:, :, 0 : LANES * HID_PASSES, :],
             )
 
-        def sort_planes(j):
+        def sort_planes(j, c):
             nc.vector.tensor_copy(
-                out=w1_planes[:, j, :, :, :].rearrange("p c t m -> p c m t"),
-                in_=w1_raw_planes[:, j, :].rearrange("p (c m t) -> p c m t", c=HID_PASSES, t=PACK),
+                out=w1_planes[:, j, c, :, :].rearrange("p t m -> p m t"),
+                in_=w1_raw_planes[:, j, c * K_PASS : (c + 1) * K_PASS].rearrange("p (m t) -> p m t", t=PACK),
             )
 
-        def sort_codes(g):
-            for c in range(HID_PASSES):
-                nc.vector.tensor_copy(
-                    out=w1_codes[:, g, c, :, :].bitcast(I32).rearrange("p t (a i) -> p a t i", i=COLS_TOGETHER),
-                    in_=w1_raw[:, g, c * K_PASS : (c + 1) * K_PASS]
-                    .bitcast(I32)
-                    .rearrange("p (a i t) -> p a t i", i=COLS_TOGETHER, t=PACK),
-                )
+        def sort_codes(g, c):
+            nc.vector.tensor_copy(
+                out=w1_codes[:, g, c, :, :].bitcast(I32).rearrange("p t (a i) -> p a t i", i=COLS_TOGETHER),
+                in_=w1_raw[:, g, c * K_PASS : (c + 1) * K_PASS]
+                .bitcast(I32)
+                .rearrange("p (a i t) -> p a t i", i=COLS_TOGETHER, t=PACK),
+            )
+
+        def sort_b2():
+            nc.vector.tensor_copy(
+                out=b2_row[0:1, :, :].rearrange("p (a i) g -> p a g i", i=COLS_TOGETHER),
+                in_=b2_raw[0:1, :, :].rearrange("p g (a i) -> p a g i", i=COLS_TOGETHER),
+            )
 
         def spread_b2(q):
             feats = slice(q * RES_FEATS, (q + 1) * RES_FEATS)
             bank = psum.tile([P, RES_FEATS, LANES], F32, tag="small", bufs=2)
             nc.tensor.matmul(
-                bank[:], lhsT=ones[:], rhs=b2_row[:, :, feats].rearrange("p g d -> p d g"), start=True, stop=True
+                bank[:], lhsT=ones[:], rhs=b2_row[:, feats, :], start=True, stop=True
             )
             return bank
 
@@ -174,7 +181,7 @@ def tile_blockresmlp_mixerblock_pa_e_kernel(
                 stop=False,
             )
             nc.tensor.matmul(
-                bank[:], lhsT=ones[:], rhs=b2_row[:, :, feats].rearrange("p g d -> p d g"), start=False, stop=True
+                bank[:], lhsT=ones[:], rhs=b2_row[:, feats, :], start=False, stop=True
             )
             nc.scalar.copy(out=result[r][:, feats, :], in_=bank[:])
 
@@ -201,8 +208,8 @@ def tile_blockresmlp_mixerblock_pa_e_kernel(
                 in_=z_grouped[:].rearrange("p g b t -> p (g b t)"),
             )
 
-        def quantise_z_tile(j, r, z_grouped):
-            for e in range(WORD_LANES):
+        def quantise_z_tile(j, r, z_grouped, lanes=range(WORD_LANES)):
+            for e in lanes:
                 nc.vector.quantize_mx(
                     out=z_codes[:, j * WORD_LANES + e, r * P : (r + 1) * P].bitcast(FP8X4),
                     scales=z_scales[:, j * WORD_LANES + e, r * P : (r + 1) * P],
@@ -267,11 +274,13 @@ def tile_blockresmlp_mixerblock_pa_e_kernel(
                 in_=h_grouped[:].rearrange("p b t -> p (b t)"),
             )
 
-        def layer2(group, r, f):
+        def layer2_bank(tag, bufs):
+            return psum.tile([P, LANE_GROUP, FEAT_CHUNK], F32, tag=tag, bufs=bufs, name="acc2")
+
+        def layer2(group, r, f, acc2, lanes=range(LANE_GROUP)):
             feats = slice(f * FEAT_CHUNK, (f + 1) * FEAT_CHUNK)
             rows = slice(r * P, (r + 1) * P)
-            acc2 = psum.tile([P, LANE_GROUP, FEAT_CHUNK], F32, tag="acc2", bufs=2)
-            for m in range(LANE_GROUP):
+            for m in lanes:
                 for c in range(HID_PASSES):
                     k_group = (group * LANE_GROUP + m) * HID_PASSES + c
                     nc.tensor.matmul_mx(
@@ -285,20 +294,23 @@ def tile_blockresmlp_mixerblock_pa_e_kernel(
                     )
             return acc2
 
-        def add_layer2(group, r, f, acc2):
-            feats = slice(f * FEAT_CHUNK, (f + 1) * FEAT_CHUNK)
+        def add_layer2(group, r, f, acc2, pieces=1):
             lanes = slice(group * LANE_GROUP, (group + 1) * LANE_GROUP)
-            nc.vector.tensor_tensor(
-                out=result[r][:, feats, lanes],
-                in0=acc2[:].rearrange("b g d -> b d g"),
-                in1=result[r][:, feats, lanes],
-                op=ALU.add,
-            )
-            if group == GROUPS - 1:
-                nc.sync.dma_start(
-                    out=out[r * P : (r + 1) * P, f * FEAT_CHUNK * LANES : (f + 1) * FEAT_CHUNK * LANES],
-                    in_=result[r][:, feats, :].rearrange("b d g -> b (d g)"),
+            width = FEAT_CHUNK // pieces
+            for at in range(0, FEAT_CHUNK, width):
+                first_feat = f * FEAT_CHUNK + at
+                feats = slice(first_feat, first_feat + width)
+                nc.vector.tensor_tensor(
+                    out=result[r][:, feats, lanes],
+                    in0=acc2[:, :, at : at + width].rearrange("b g d -> b d g"),
+                    in1=result[r][:, feats, lanes],
+                    op=ALU.add,
                 )
+                if group == GROUPS - 1:
+                    nc.sync.dma_start(
+                        out=out[r * P : (r + 1) * P, first_feat * LANES : (first_feat + width) * LANES],
+                        in_=result[r][:, feats, :].rearrange("b d g -> b (d g)"),
+                    )
 
         both = slice(0, ROWS)
         tiles = [slice(r * P, (r + 1) * P) for r in range(ROW_TILES)]
@@ -318,24 +330,36 @@ def tile_blockresmlp_mixerblock_pa_e_kernel(
         chunks = [(group, r, f) for group in range(GROUPS) for r in range(ROW_TILES) for f in range(FEAT_CHUNKS)]
         residuals = [(r, q) for r in range(ROW_TILES) for q in range(RES_CHUNKS)]
 
+        def steps_are_long(i):
+            return i < len(steps) and steps[i][2] == both
+
         def new_z(width):
             return work.tile([P, WORD_LANES, width, PACK], BF16, tag="z_grouped", bufs=2, align_bytes=64, name="z_grouped")
 
-        bias_columns()
-        sort_planes(0)
+        zt_first = transpose_z(0, 0)
         z_first = new_z(P)
-        copy_z(transpose_z(0, 0), z_first, 0)
-        sort_codes(0)
+        copy_z(zt_first, z_first, 0)
+        sort_b2()
+        sort_planes(0, 0)
+        sort_codes(0, 0)
+        bias_columns()
         for q in range(HEAD_RESIDUALS):
             residual_by_matmul(*residuals.pop(0))
-        quantise_z_tile(0, 0, z_first)
+        quantise_z_tile(0, 0, z_first, (0,))
         sums_ahead = layer1(steps[0])
+        sort_planes(0, 1)
+        sort_codes(0, 1)
+        quantise_z_tile(0, 0, z_first, (1,))
         zt = transpose_z(0, 1)
         by_scalar = [residuals.pop(0) for q in range(STEP_RESIDUALS)]
         b2_ahead = spread_b2(residuals[0][1])
         parts_before = None
         z_waiting = None
         z_tile_one = None
+        adds = []
+        tail = [(GROUPS - 1, ROW_TILES - 1, f) for f in range(FEAT_CHUNKS)]
+        chunks = [ch for ch in chunks if ch not in tail]
+        tail_banks = []
         for i in range(len(steps) + 1):
             sums = sums_ahead
             if i == 0:
@@ -343,10 +367,13 @@ def tile_blockresmlp_mixerblock_pa_e_kernel(
             if i + 1 < len(steps):
                 sums_ahead = layer1(steps[i + 1])
             ready = [ch for ch in chunks if last(ch[0], ch[1]) + 2 <= i]
-            chunk = ready[0] if ready else None
-            if chunk:
+            for chunk in ready[: 2 if steps_are_long(i) or i == len(steps) - 1 else 1]:
                 chunks.remove(chunk)
-                acc2 = layer2(*chunk)
+                adds.append((chunk, layer2(*chunk, layer2_bank("acc2", 2))))
+            if i == len(steps) - 1:
+                for f, chunk in enumerate(tail):
+                    bank = layer2_bank("small", 2) if f < 2 else layer2_bank("acc1", 4)
+                    tail_banks.append(layer2(*chunk, bank, range(LANE_GROUP - 1)))
             parts = exp_and_relu(steps[i], sums) if i < len(steps) else None
             h_grouped = elu(steps[i - 1], parts_before) if i >= 1 else None
             parts_before = parts
@@ -366,10 +393,13 @@ def tile_blockresmlp_mixerblock_pa_e_kernel(
                     quantise_z(j, z_waiting)
             for g in range(1, LANES):
                 if i == first[g] - 3:
-                    sort_codes(g)
+                    for c in range(HID_PASSES):
+                        sort_codes(g, c)
             if i == first[LANE_GROUP] - 4:
-                sort_planes(1)
-            if chunk:
+                for c in range(HID_PASSES):
+                    sort_planes(1, c)
+            for chunk, acc2 in adds[: 2 if steps_are_long(i) else 1]:
+                adds.remove((chunk, acc2))
                 add_layer2(*chunk, acc2)
             if residuals:
                 residual_plus_bias(*residuals.pop(0), b2_ahead)
@@ -377,5 +407,6 @@ def tile_blockresmlp_mixerblock_pa_e_kernel(
                     b2_ahead = spread_b2(residuals[0][1])
             if i >= 1:
                 quantise_h(steps[i - 1], h_grouped)
-        for chunk in chunks:
-            add_layer2(*chunk, layer2(*chunk))
+        for chunk, bank in zip(tail, tail_banks):
+            layer2(*chunk, bank, (LANE_GROUP - 1,))
+            add_layer2(*chunk, bank, 2 if chunk == tail[-1] else 1)

@@ -32,8 +32,8 @@ K_STEP = PACK * PAIRS
 QUADRANTS = 4
 RES_FEATS = BANK // LANES
 RES_CHUNKS = BLOCK // RES_FEATS
-HEAD_RESIDUALS = 2
-STEP_RESIDUALS = 7
+HEAD_RESIDUALS = 4
+SCALAR_FROM = 4
 COLS_TOGETHER = 4
 
 FLOPS = 2 * LANES * ROWS * (BLOCK * HID + HID * BLOCK)
@@ -106,11 +106,11 @@ def tile_blockresmlp_mixerblock_pa_e_kernel(
         nc.scalar.dma_start(
             out=b2_raw[0:1, :, :].rearrange("p g n -> p (g n)"), in_=b2.rearrange("g o n -> o (g n)")
         )
-        load_y(0)
-        load_planes(w1_raw_planes, w1_scales, 0)
-        nc.sync.dma_start(
+        nc.scalar.dma_start(
             out=b1_rows[0 : LANES * HID_PASSES, :], in_=b1.rearrange("g o (c n) -> (g o c) n", c=HID_PASSES)
         )
+        load_y(0)
+        load_planes(w1_raw_planes, w1_scales, 0)
         for c in range(HID_PASSES):
             load_w1(0, slice(c * K_PASS, (c + 1) * K_PASS))
         load_y(1)
@@ -153,9 +153,9 @@ def tile_blockresmlp_mixerblock_pa_e_kernel(
                 in_=b2_raw[0:1, :, :].rearrange("p g (a i) -> p a g i", i=COLS_TOGETHER),
             )
 
-        def spread_b2(q):
+        def spread_b2(q, tag):
             feats = slice(q * RES_FEATS, (q + 1) * RES_FEATS)
-            bank = psum.tile([P, RES_FEATS, LANES], F32, tag="small", bufs=2)
+            bank = psum.tile([P, RES_FEATS, LANES], F32, tag=tag, bufs=2)
             nc.tensor.matmul(
                 bank[:], lhsT=ones[:], rhs=b2_row[:, feats, :], start=True, stop=True
             )
@@ -170,9 +170,9 @@ def tile_blockresmlp_mixerblock_pa_e_kernel(
                 op=ALU.add,
             )
 
-        def residual_by_matmul(r, q):
+        def residual_by_matmul(r, q, tag):
             feats = slice(q * RES_FEATS, (q + 1) * RES_FEATS)
-            bank = psum.tile([P, RES_FEATS, LANES], F32, tag="acc2", bufs=2)
+            bank = psum.tile([P, RES_FEATS, LANES], F32, tag=tag, bufs=2)
             nc.tensor.matmul(
                 bank[:],
                 lhsT=ident_bf16[:],
@@ -328,7 +328,7 @@ def tile_blockresmlp_mixerblock_pa_e_kernel(
             )
 
         chunks = [(group, r, f) for group in range(GROUPS) for r in range(ROW_TILES) for f in range(FEAT_CHUNKS)]
-        residuals = [(r, q) for r in range(ROW_TILES) for q in range(RES_CHUNKS)]
+        by_scalar = [(0, q) for q in range(6)] + [(1, q) for q in range(5)]
 
         def steps_are_long(i):
             return i < len(steps) and steps[i][2] == both
@@ -336,23 +336,22 @@ def tile_blockresmlp_mixerblock_pa_e_kernel(
         def new_z(width):
             return work.tile([P, WORD_LANES, width, PACK], BF16, tag="z_grouped", bufs=2, align_bytes=64, name="z_grouped")
 
-        zt_first = transpose_z(0, 0)
-        z_first = new_z(P)
-        copy_z(zt_first, z_first, 0)
+        bias_columns()
         sort_b2()
+        z_first = new_z(P)
+        copy_z(transpose_z(0, 0), z_first, 0)
         sort_planes(0, 0)
         sort_codes(0, 0)
-        bias_columns()
         for q in range(HEAD_RESIDUALS):
-            residual_by_matmul(*residuals.pop(0))
+            residual_by_matmul(*by_scalar.pop(0), "acc2" if q % 2 else "small")
         quantise_z_tile(0, 0, z_first, (0,))
         sums_ahead = layer1(steps[0])
         sort_planes(0, 1)
         sort_codes(0, 1)
         quantise_z_tile(0, 0, z_first, (1,))
-        zt = transpose_z(0, 1)
-        by_scalar = [residuals.pop(0) for q in range(STEP_RESIDUALS)]
-        b2_ahead = spread_b2(residuals[0][1])
+        banks = [(q, spread_b2(q, "acc2")) for q in (6, 7)]
+        for q, bank in banks:
+            residual_plus_bias(0, q, bank)
         parts_before = None
         z_waiting = None
         z_tile_one = None
@@ -378,10 +377,10 @@ def tile_blockresmlp_mixerblock_pa_e_kernel(
             h_grouped = elu(steps[i - 1], parts_before) if i >= 1 else None
             parts_before = parts
             if i == 0:
-                copy_z(zt, z_tile_one, 0)
+                copy_z(transpose_z(0, 1), z_tile_one, 0)
                 quantise_z_tile(0, 1, z_tile_one)
-            if by_scalar:
-                residual_by_matmul(*by_scalar.pop(0))
+            if by_scalar and i >= SCALAR_FROM:
+                residual_by_matmul(*by_scalar.pop(0), "small")
             for j in range(1, PAIRS):
                 start = first[j * WORD_LANES] - 4
                 if i == start:
@@ -392,19 +391,19 @@ def tile_blockresmlp_mixerblock_pa_e_kernel(
                 if i == start + 2:
                     quantise_z(j, z_waiting)
             for g in range(1, LANES):
-                if i == first[g] - 3:
+                if i == g:
                     for c in range(HID_PASSES):
                         sort_codes(g, c)
-            if i == first[LANE_GROUP] - 4:
+            if i == LANES - 1:
                 for c in range(HID_PASSES):
                     sort_planes(1, c)
             for chunk, acc2 in adds[: 2 if steps_are_long(i) else 1]:
                 adds.remove((chunk, acc2))
                 add_layer2(*chunk, acc2)
-            if residuals:
-                residual_plus_bias(*residuals.pop(0), b2_ahead)
-                if residuals:
-                    b2_ahead = spread_b2(residuals[0][1])
+            if i == 0:
+                for q, bank in banks:
+                    residual_plus_bias(1, q, bank)
+                residual_plus_bias(1, 5, spread_b2(5, "small"))
             if i >= 1:
                 quantise_h(steps[i - 1], h_grouped)
         for chunk, bank in zip(tail, tail_banks):

@@ -32,8 +32,10 @@ K_STEP = PACK * PAIRS
 QUADRANTS = 4
 RES_FEATS = BANK // LANES
 RES_CHUNKS = BLOCK // RES_FEATS
-HEAD_RESIDUALS = 4
+HEAD_RESIDUALS = 2
 SCALAR_FROM = 4
+V_RELU = (3,)
+V_STEPS = range(6, 11)
 COLS_TOGETHER = 4
 
 FLOPS = 2 * LANES * ROWS * (BLOCK * HID + HID * BLOCK)
@@ -237,7 +239,7 @@ def tile_blockresmlp_mixerblock_pa_e_kernel(
                 )
             return sums
 
-        def exp_and_relu(step, sums):
+        def exp_and_relu(step, sums, on_vector):
             g, c, rows = step
             width = rows.stop - rows.start
             e = work.tile([P, PACK, width], F32, tag="e", bufs=3)
@@ -248,12 +250,17 @@ def tile_blockresmlp_mixerblock_pa_e_kernel(
 
             for t in range(PACK):
                 nc.scalar.activation(out=e[:, t, :], in_=sums[t], func=ACT.Exp, bias=bias(t))
-                nc.scalar.activation(out=pos[:, t, :], in_=sums[t], func=ACT.Relu, bias=bias(t))
-            return e, pos
+                if t not in on_vector:
+                    nc.scalar.activation(out=pos[:, t, :], in_=sums[t], func=ACT.Relu, bias=bias(t))
+            return e, pos, [(pos, t, sums[t], bias(t)) for t in on_vector]
 
         def elu(step, parts):
             g, c, rows = step
-            e, pos = parts
+            e, pos, rest = parts
+            for tile, t, total, bias in rest:
+                nc.vector.tensor_scalar(
+                    out=tile[:, t, :], in0=total, scalar1=bias, scalar2=0.0, op0=ALU.add, op1=ALU.max
+                )
             h_grouped = work.tile([P, rows.stop - rows.start, PACK], BF16, tag="h_grouped", bufs=3, align_bytes=64)
             nc.vector.scalar_tensor_tensor(
                 out=h_grouped[:],
@@ -336,33 +343,44 @@ def tile_blockresmlp_mixerblock_pa_e_kernel(
         def new_z(width):
             return work.tile([P, WORD_LANES, width, PACK], BF16, tag="z_grouped", bufs=2, align_bytes=64, name="z_grouped")
 
-        bias_columns()
         sort_b2()
         z_first = new_z(P)
         copy_z(transpose_z(0, 0), z_first, 0)
         sort_planes(0, 0)
         sort_codes(0, 0)
+        bias_columns()
         for q in range(HEAD_RESIDUALS):
-            residual_by_matmul(*by_scalar.pop(0), "acc2" if q % 2 else "small")
+            residual_by_matmul(*by_scalar.pop(0), "acc2")
         quantise_z_tile(0, 0, z_first, (0,))
-        sums_ahead = layer1(steps[0])
+        sums = layer1(steps[0])
         sort_planes(0, 1)
         sort_codes(0, 1)
         quantise_z_tile(0, 0, z_first, (1,))
+        sums_ahead = layer1(steps[1])
         banks = [(q, spread_b2(q, "acc2")) for q in (6, 7)]
+        z_second = new_z(P)
+        zt = transpose_z(0, 1)
+        parts = exp_and_relu(steps[0], sums, ())
+        residual_plus_bias(0, *banks[0])
+        h_grouped = elu(steps[0], parts)
+        residual_plus_bias(0, *banks[1])
+        parts_before = exp_and_relu(steps[1], sums_ahead, ())
+        copy_z(zt, z_second, 0)
+        residual_by_matmul(*by_scalar.pop(0), "small")
+        quantise_z_tile(0, 1, z_second)
+        quantise_h(steps[0], h_grouped)
+        sums_ahead = layer1(steps[2])
         for q, bank in banks:
-            residual_plus_bias(0, q, bank)
-        parts_before = None
+            residual_plus_bias(1, q, bank)
+        sort_codes(1, 0)
+        sort_codes(1, 1)
         z_waiting = None
-        z_tile_one = None
         adds = []
         tail = [(GROUPS - 1, ROW_TILES - 1, f) for f in range(FEAT_CHUNKS)]
         chunks = [ch for ch in chunks if ch not in tail]
         tail_banks = []
-        for i in range(len(steps) + 1):
+        for i in range(2, len(steps) + 1):
             sums = sums_ahead
-            if i == 0:
-                z_tile_one = new_z(P)
             if i + 1 < len(steps):
                 sums_ahead = layer1(steps[i + 1])
             ready = [ch for ch in chunks if last(ch[0], ch[1]) + 2 <= i]
@@ -373,12 +391,9 @@ def tile_blockresmlp_mixerblock_pa_e_kernel(
                 for f, chunk in enumerate(tail):
                     bank = layer2_bank("small", 2) if f < 2 else layer2_bank("acc1", 4)
                     tail_banks.append(layer2(*chunk, bank, range(LANE_GROUP - 1)))
-            parts = exp_and_relu(steps[i], sums) if i < len(steps) else None
-            h_grouped = elu(steps[i - 1], parts_before) if i >= 1 else None
+            parts = exp_and_relu(steps[i], sums, V_RELU if i in V_STEPS else ()) if i < len(steps) else None
+            h_grouped = elu(steps[i - 1], parts_before)
             parts_before = parts
-            if i == 0:
-                copy_z(transpose_z(0, 1), z_tile_one, 0)
-                quantise_z_tile(0, 1, z_tile_one)
             if by_scalar and i >= SCALAR_FROM:
                 residual_by_matmul(*by_scalar.pop(0), "small")
             for j in range(1, PAIRS):
@@ -390,7 +405,7 @@ def tile_blockresmlp_mixerblock_pa_e_kernel(
                     copy_z(transpose_z(j, 1), z_waiting, P)
                 if i == start + 2:
                     quantise_z(j, z_waiting)
-            for g in range(1, LANES):
+            for g in range(2, LANES):
                 if i == g:
                     for c in range(HID_PASSES):
                         sort_codes(g, c)
@@ -400,12 +415,9 @@ def tile_blockresmlp_mixerblock_pa_e_kernel(
             for chunk, acc2 in adds[: 2 if steps_are_long(i) else 1]:
                 adds.remove((chunk, acc2))
                 add_layer2(*chunk, acc2)
-            if i == 0:
-                for q, bank in banks:
-                    residual_plus_bias(1, q, bank)
+            if i == 2:
                 residual_plus_bias(1, 5, spread_b2(5, "small"))
-            if i >= 1:
-                quantise_h(steps[i - 1], h_grouped)
+            quantise_h(steps[i - 1], h_grouped)
         for chunk, bank in zip(tail, tail_banks):
             layer2(*chunk, bank, (LANE_GROUP - 1,))
             add_layer2(*chunk, bank, 2 if chunk == tail[-1] else 1)

@@ -34,7 +34,7 @@ RES_FEATS = BANK // LANES
 RES_CHUNKS = BLOCK // RES_FEATS
 HEAD_RESIDUALS = 2
 SCALAR_FROM = 4
-V_RELU = (3,)
+V_RELU = (2, 3)
 V_STEPS = range(6, 11)
 COLS_TOGETHER = 4
 
@@ -55,6 +55,7 @@ def tile_blockresmlp_mixerblock_pa_e_kernel(
         ident_bf16 = keep.tile([P, P], BF16)
         ones = keep.tile([P, P], BF16)
         warm = keep.tile([P, 1], F32)
+        idle = keep.tile([P, 2 * P], F32)
         b1_rows = keep.tile([P, BLOCK], BF16, align_bytes=64)
         b1_cols = keep.tile([P, LANES * HID_PASSES, PACK], F32)
         b2_raw = keep.tile([P, LANES, BLOCK], BF16)
@@ -75,6 +76,7 @@ def tile_blockresmlp_mixerblock_pa_e_kernel(
         nc.vector.memset(warm[:], 0.0)
         nc.vector.memset(w1_raw_planes[:].bitcast(I32), 0)
         nc.vector.memset(b2_row[:].bitcast(I32), 0)
+        nc.vector.memset(idle[:], 0.0)
         nc.vector.memset(w2_planes[:].bitcast(I32), 0)
         nc.vector.memset(ones[:], 1.0)
         nc.scalar.activation(out=warm[:], in_=warm[:], func=ACT.Exp)
@@ -124,6 +126,10 @@ def tile_blockresmlp_mixerblock_pa_e_kernel(
             load_planes(w2_planes, w2_scales, j)
         for g in range(LANES):
             load_w2(g)
+
+        def warm_up():
+            bank = psum.tile([P, 2 * P], F32, tag="acc1", bufs=4)
+            nc.tensor.matmul(bank[:], lhsT=ident[:], rhs=idle[:], start=True, stop=True)
 
         def bias_columns():
             words = b1_rows[:].bitcast(F32)
@@ -254,13 +260,15 @@ def tile_blockresmlp_mixerblock_pa_e_kernel(
                     nc.scalar.activation(out=pos[:, t, :], in_=sums[t], func=ACT.Relu, bias=bias(t))
             return e, pos, [(pos, t, sums[t], bias(t)) for t in on_vector]
 
-        def elu(step, parts):
-            g, c, rows = step
-            e, pos, rest = parts
-            for tile, t, total, bias in rest:
+        def relu_by_vector(parts):
+            for tile, t, total, bias in parts[2]:
                 nc.vector.tensor_scalar(
                     out=tile[:, t, :], in0=total, scalar1=bias, scalar2=0.0, op0=ALU.add, op1=ALU.max
                 )
+
+        def elu(step, parts):
+            g, c, rows = step
+            e, pos, rest = parts
             h_grouped = work.tile([P, rows.stop - rows.start, PACK], BF16, tag="h_grouped", bufs=3, align_bytes=64)
             nc.vector.scalar_tensor_tensor(
                 out=h_grouped[:],
@@ -343,19 +351,19 @@ def tile_blockresmlp_mixerblock_pa_e_kernel(
         def new_z(width):
             return work.tile([P, WORD_LANES, width, PACK], BF16, tag="z_grouped", bufs=2, align_bytes=64, name="z_grouped")
 
+        warm_up()
         sort_b2()
         z_first = new_z(P)
         copy_z(transpose_z(0, 0), z_first, 0)
-        sort_planes(0, 0)
-        sort_codes(0, 0)
         bias_columns()
         for q in range(HEAD_RESIDUALS):
             residual_by_matmul(*by_scalar.pop(0), "acc2")
-        quantise_z_tile(0, 0, z_first, (0,))
+        quantise_z_tile(0, 0, z_first)
+        sort_planes(0, 0)
+        sort_codes(0, 0)
         sums = layer1(steps[0])
         sort_planes(0, 1)
         sort_codes(0, 1)
-        quantise_z_tile(0, 0, z_first, (1,))
         sums_ahead = layer1(steps[1])
         banks = [(q, spread_b2(q, "acc2")) for q in (6, 7)]
         z_second = new_z(P)
@@ -375,6 +383,9 @@ def tile_blockresmlp_mixerblock_pa_e_kernel(
         sort_codes(1, 0)
         sort_codes(1, 1)
         z_waiting = None
+        sorting = {g: (sort_codes, g) for g in range(2, LANES - 1)}
+        sorting[LANES - 1] = (sort_planes, 1)
+        sorting[LANES] = (sort_codes, LANES - 1)
         adds = []
         tail = [(GROUPS - 1, ROW_TILES - 1, f) for f in range(FEAT_CHUNKS)]
         chunks = [ch for ch in chunks if ch not in tail]
@@ -383,8 +394,11 @@ def tile_blockresmlp_mixerblock_pa_e_kernel(
             sums = sums_ahead
             if i + 1 < len(steps):
                 sums_ahead = layer1(steps[i + 1])
+            relu_by_vector(parts_before)
+            if i >= 3:
+                quantise_h(steps[i - 2], h_grouped)
             ready = [ch for ch in chunks if last(ch[0], ch[1]) + 2 <= i]
-            for chunk in ready[: 2 if steps_are_long(i) or i == len(steps) - 1 else 1]:
+            for chunk in ready[: 2 if i == len(steps) - 1 else 1]:
                 chunks.remove(chunk)
                 adds.append((chunk, layer2(*chunk, layer2_bank("acc2", 2))))
             if i == len(steps) - 1:
@@ -392,8 +406,6 @@ def tile_blockresmlp_mixerblock_pa_e_kernel(
                     bank = layer2_bank("small", 2) if f < 2 else layer2_bank("acc1", 4)
                     tail_banks.append(layer2(*chunk, bank, range(LANE_GROUP - 1)))
             parts = exp_and_relu(steps[i], sums, V_RELU if i in V_STEPS else ()) if i < len(steps) else None
-            h_grouped = elu(steps[i - 1], parts_before)
-            parts_before = parts
             if by_scalar and i >= SCALAR_FROM:
                 residual_by_matmul(*by_scalar.pop(0), "small")
             for j in range(1, PAIRS):
@@ -403,21 +415,21 @@ def tile_blockresmlp_mixerblock_pa_e_kernel(
                     copy_z(transpose_z(j, 0), z_waiting, 0)
                 if i == start + 1:
                     copy_z(transpose_z(j, 1), z_waiting, P)
-                if i == start + 2:
+            h_grouped = elu(steps[i - 1], parts_before)
+            parts_before = parts
+            for j in range(1, PAIRS):
+                if i == first[j * WORD_LANES] - 2:
                     quantise_z(j, z_waiting)
-            for g in range(2, LANES):
-                if i == g:
-                    for c in range(HID_PASSES):
-                        sort_codes(g, c)
-            if i == LANES - 1:
+            if i in sorting:
+                sort, what = sorting[i]
                 for c in range(HID_PASSES):
-                    sort_planes(1, c)
-            for chunk, acc2 in adds[: 2 if steps_are_long(i) else 1]:
+                    sort(what, c)
+            for chunk, acc2 in adds[:1]:
                 adds.remove((chunk, acc2))
                 add_layer2(*chunk, acc2)
             if i == 2:
                 residual_plus_bias(1, 5, spread_b2(5, "small"))
-            quantise_h(steps[i - 1], h_grouped)
+        quantise_h(steps[-1], h_grouped)
         for chunk, bank in zip(tail, tail_banks):
             layer2(*chunk, bank, (LANE_GROUP - 1,))
-            add_layer2(*chunk, bank, 2 if chunk == tail[-1] else 1)
+            add_layer2(*chunk, bank, 2 if chunk == tail[0] else 1)

from contextlib import ExitStack

import concourse.mybir as mybir
from concourse.masks import make_identity

F32 = mybir.dt.float32
BF16 = mybir.dt.bfloat16
I32 = mybir.dt.int32
U32 = mybir.dt.uint32
U8 = mybir.dt.uint8
FP8X4 = mybir.dt.float8_e4m3fn_x4
ALU = mybir.AluOpType
ACT = mybir.ActivationFunctionType

P = 128
PACK = 4
K_PASS = P * PACK
BANK = 512
LANES = 8
BLOCK = 512
HID = 1024
ROWS = 256
ROW_TILES = ROWS // P
HID_PASSES = HID // K_PASS
LANE_GROUP = 4
GROUPS = LANES // LANE_GROUP
FEAT_CHUNK = P
FEAT_CHUNKS = BLOCK // FEAT_CHUNK
WORD_LANES = 2
PAIRS = LANES // WORD_LANES
K_STEP = PACK * PAIRS
QUADRANTS = 4
RES_FEATS = BANK // LANES
RES_CHUNKS = BLOCK // RES_FEATS
HEAD_RESIDUALS = 2
SCALAR_FROM = 4
V_RELU = (2, 3)
V_STEPS = range(6, 11)
COLS_TOGETHER = 4

FLOPS = 2 * LANES * ROWS * (BLOCK * HID + HID * BLOCK)


def tile_blockresmlp_mixerblock_pa_e_kernel(
    tc, y_lanes, w1_words, w1_scales, b1, w2_words, w2_scales, b2, out
):
    nc = tc.nc
    with ExitStack() as ctx:
        keep = ctx.enter_context(tc.tile_pool(name="keep", bufs=1))
        work = ctx.enter_context(tc.tile_pool(name="work", bufs=2))
        psum = ctx.enter_context(tc.psum_pool(name="psum", bufs=2))
        ctx.enter_context(tc.manual_schedule())

        ident = keep.tile([P, P], F32)
        ident_bf16 = keep.tile([P, P], BF16)
        ones = keep.tile([P, P], BF16)
        warm = keep.tile([P, 1], F32)
        idle = keep.tile([P, 2 * P], F32)
        b1_rows = keep.tile([P, BLOCK], BF16, align_bytes=64)
        b1_cols = keep.tile([P, LANES * HID_PASSES, PACK], F32)
        b2_raw = keep.tile([P, LANES, BLOCK], BF16)
        b2_row = keep.tile([P, BLOCK, LANES], BF16)
        y_sb = [keep.tile([P, BLOCK * LANES], BF16, name="y%d" % r) for r in range(ROW_TILES)]
        w1_raw = keep.tile([P, LANES, HID], U32, align_bytes=64)
        w1_codes = keep.tile([P, LANES, HID_PASSES, PACK, P], U32, align_bytes=64)
        w1_raw_planes = keep.tile([P, GROUPS, HID], U8, align_bytes=64)
        w1_planes = keep.tile([P, GROUPS, HID_PASSES, PACK, P], U8, align_bytes=64)
        w2_codes = keep.tile([P, LANES * HID_PASSES, BLOCK], U32, align_bytes=64)
        w2_planes = keep.tile([P, GROUPS * HID_PASSES, BLOCK], U8, align_bytes=64)
        result = [keep.tile([P, BLOCK, LANES], F32, name="result%d" % r) for r in range(ROW_TILES)]
        z_codes = keep.tile([P, LANES, ROWS], U32, align_bytes=64)
        z_scales = keep.tile([P, LANES, ROWS], U8, align_bytes=64)
        h_codes = keep.tile([P, LANES * HID_PASSES, ROWS], U32, align_bytes=64)
        h_scales = keep.tile([P, LANES * HID_PASSES, ROWS], U8, align_bytes=64)

        nc.vector.memset(warm[:], 0.0)
        nc.vector.memset(w1_raw_planes[:].bitcast(I32), 0)
        nc.vector.memset(b2_row[:].bitcast(I32), 0)
        nc.vector.memset(idle[:], 0.0)
        nc.vector.memset(w2_planes[:].bitcast(I32), 0)
        nc.vector.memset(ones[:], 1.0)
        nc.scalar.activation(out=warm[:], in_=warm[:], func=ACT.Exp)
        nc.gpsimd.memset(b1_rows[:].bitcast(I32), 0)
        make_identity(nc, ident[:])
        nc.vector.tensor_copy(out=ident_bf16[:], in_=ident[:])

        def load_y(r):
            nc.sync.dma_start(out=y_sb[r][:], in_=y_lanes[r * P : (r + 1) * P, :])

        def load_planes(planes, scales, j):
            for quad in range(QUADRANTS):
                nc.sync.dma_start(
                    out=planes[32 * quad : 32 * quad + 16, j, :].bitcast(I32),
                    in_=scales[4 * j : 4 * j + 4, 4 * quad : 4 * quad + 4, :].bitcast(I32),
                )

        def load_w1(g, columns=slice(0, HID)):
            nc.sync.dma_start(
                out=w1_raw[:, g, columns].bitcast(I32),
                in_=w1_words[g][:, columns, :].rearrange("p n t -> p (n t)").bitcast(I32),
            )

        def load_w2(g):
            passes = slice(g * HID_PASSES, (g + 1) * HID_PASSES)
            nc.sync.dma_start(
                out=w2_codes[:, passes, :].bitcast(I32),
                in_=w2_words[passes].rearrange("c p n t -> p c (n t)").bitcast(I32),
            )

        nc.scalar.dma_start(
            out=b2_raw[0:1, :, :].rearrange("p g n -> p (g n)"), in_=b2.rearrange("g o n -> o (g n)")
        )
        nc.scalar.dma_start(
            out=b1_rows[0 : LANES * HID_PASSES, :], in_=b1.rearrange("g o (c n) -> (g o c) n", c=HID_PASSES)
        )
        load_y(0)
        load_planes(w1_raw_planes, w1_scales, 0)
        for c in range(HID_PASSES):
            load_w1(0, slice(c * K_PASS, (c + 1) * K_PASS))
        load_y(1)
        load_w1(1)
        load_planes(w1_raw_planes, w1_scales, 1)
        for g in range(2, LANES):
            load_w1(g)
        for j in range(GROUPS * HID_PASSES):
            load_planes(w2_planes, w2_scales, j)
        for g in range(LANES):
            load_w2(g)

        def warm_up():
            bank = psum.tile([P, 2 * P], F32, tag="acc1", bufs=4)
            nc.tensor.matmul(bank[:], lhsT=ident[:], rhs=idle[:], start=True, stop=True)

        def bias_columns():
            words = b1_rows[:].bitcast(F32)
            bank = psum.tile([P, 2, P], F32, tag="small", bufs=2)
            for u in range(2):
                nc.tensor.transpose(bank[:, u, :], words[:, u : BLOCK // 2 : 2], ident[:])
            nc.vector.tensor_copy(
                out=b1_cols[:].rearrange("p r (u e) -> p u r e", e=2),
                in_=bank[:].bitcast(BF16).rearrange("p u (r e) -> p u r e", e=2)[:, :, 0 : LANES * HID_PASSES, :],
            )

        def sort_planes(j, c):
            nc.vector.tensor_copy(
                out=w1_planes[:, j, c, :, :].rearrange("p t m -> p m t"),
                in_=w1_raw_planes[:, j, c * K_PASS : (c + 1) * K_PASS].rearrange("p (m t) -> p m t", t=PACK),
            )

        def sort_codes(g, c):
            nc.vector.tensor_copy(
                out=w1_codes[:, g, c, :, :].bitcast(I32).rearrange("p t (a i) -> p a t i", i=COLS_TOGETHER),
                in_=w1_raw[:, g, c * K_PASS : (c + 1) * K_PASS]
                .bitcast(I32)
                .rearrange("p (a i t) -> p a t i", i=COLS_TOGETHER, t=PACK),
            )

        def sort_b2():
            nc.vector.tensor_copy(
                out=b2_row[0:1, :, :].rearrange("p (a i) g -> p a g i", i=COLS_TOGETHER),
                in_=b2_raw[0:1, :, :].rearrange("p g (a i) -> p a g i", i=COLS_TOGETHER),
            )

        def spread_b2(q, tag):
            feats = slice(q * RES_FEATS, (q + 1) * RES_FEATS)
            bank = psum.tile([P, RES_FEATS, LANES], F32, tag=tag, bufs=2)
            nc.tensor.matmul(
                bank[:], lhsT=ones[:], rhs=b2_row[:, feats, :], start=True, stop=True
            )
            return bank

        def residual_plus_bias(r, q, bank):
            feats = slice(q * RES_FEATS, (q + 1) * RES_FEATS)
            nc.vector.tensor_tensor(
                out=result[r][:, feats, :],
                in0=bank[:],
                in1=y_sb[r][:].rearrange("b (d g) -> b d g", g=LANES)[:, feats, :],
                op=ALU.add,
            )

        def residual_by_matmul(r, q, tag):
            feats = slice(q * RES_FEATS, (q + 1) * RES_FEATS)
            bank = psum.tile([P, RES_FEATS, LANES], F32, tag=tag, bufs=2)
            nc.tensor.matmul(
                bank[:],
                lhsT=ident_bf16[:],
                rhs=y_sb[r][:].rearrange("b (d g) -> b d g", g=LANES)[:, feats, :],
                start=True,
                stop=False,
            )
            nc.tensor.matmul(
                bank[:], lhsT=ones[:], rhs=b2_row[:, feats, :], start=False, stop=True
            )
            nc.scalar.copy(out=result[r][:, feats, :], in_=bank[:])

        def transpose_z(j, r):
            y_words = y_sb[r][:].bitcast(F32)
            zt = psum.tile([P, PACK, P], F32, tag="small", bufs=2)
            for t in range(PACK):
                first = t * PAIRS + j
                nc.tensor.transpose(zt[:, t, :], y_words[:, first : BLOCK * PAIRS : K_STEP], ident[:])
            return zt

        def copy_z(zt, z_grouped, at):
            for e in range(WORD_LANES):
                nc.scalar.copy(
                    out=z_grouped[:, e, at : at + P, :],
                    in_=zt[:].bitcast(BF16).rearrange("p t (b e) -> p e b t", e=WORD_LANES)[:, e, :, :],
                )

        def quantise_z(j, z_grouped):
            lanes = slice(j * WORD_LANES, (j + 1) * WORD_LANES)
            nc.vector.quantize_mx(
                out=z_codes[:, lanes, :].rearrange("p g b -> p (g b)").bitcast(FP8X4),
                scales=z_scales[:, lanes, :].rearrange("p g b -> p (g b)"),
                in_=z_grouped[:].rearrange("p g b t -> p (g b t)"),
            )

        def quantise_z_tile(j, r, z_grouped, lanes=range(WORD_LANES)):
            for e in lanes:
                nc.vector.quantize_mx(
                    out=z_codes[:, j * WORD_LANES + e, r * P : (r + 1) * P].bitcast(FP8X4),
                    scales=z_scales[:, j * WORD_LANES + e, r * P : (r + 1) * P],
                    in_=z_grouped[:, e, :, :].rearrange("p b t -> p (b t)"),
                )

        def layer1(step):
            g, c, rows = step
            width = rows.stop - rows.start
            per_bank = BANK // width
            plane = 4 * (g % LANE_GROUP)
            sums = []
            for t in range(PACK):
                if t % per_bank == 0:
                    acc1 = psum.tile([P, per_bank, width], F32, tag="acc1", bufs=4)
                sums.append(acc1[:, t % per_bank, :])
                nc.tensor.matmul_mx(
                    out=sums[t],
                    lhsT=w1_codes[:, g, c, t, :].bitcast(FP8X4),
                    lhsT_scale=w1_planes[plane:P, g // LANE_GROUP, c, t, :],
                    rhs=z_codes[:, g, rows].bitcast(FP8X4),
                    rhs_scale=z_scales[:, g, rows],
                    start=True,
                    stop=True,
                )
            return sums

        def exp_and_relu(step, sums, on_vector):
            g, c, rows = step
            width = rows.stop - rows.start
            e = work.tile([P, PACK, width], F32, tag="e", bufs=3)
            pos = work.tile([P, PACK, width], BF16, tag="pos", bufs=3)

            def bias(t):
                return b1_cols[:, g * HID_PASSES + c, t : t + 1]

            for t in range(PACK):
                nc.scalar.activation(out=e[:, t, :], in_=sums[t], func=ACT.Exp, bias=bias(t))
                if t not in on_vector:
                    nc.scalar.activation(out=pos[:, t, :], in_=sums[t], func=ACT.Relu, bias=bias(t))
            return e, pos, [(pos, t, sums[t], bias(t)) for t in on_vector]

        def relu_by_vector(parts):
            for tile, t, total, bias in parts[2]:
                nc.vector.tensor_scalar(
                    out=tile[:, t, :], in0=total, scalar1=bias, scalar2=0.0, op0=ALU.add, op1=ALU.max
                )

        def elu(step, parts):
            g, c, rows = step
            e, pos, rest = parts
            h_grouped = work.tile([P, rows.stop - rows.start, PACK], BF16, tag="h_grouped", bufs=3, align_bytes=64)
            nc.vector.scalar_tensor_tensor(
                out=h_grouped[:],
                in0=e[:].rearrange("p t b -> p b t"),
                scalar=-1.0,
                in1=pos[:].rearrange("p t b -> p b t"),
                op0=ALU.add,
                op1=ALU.min,
            )
            return h_grouped

        def quantise_h(step, h_grouped):
            g, c, rows = step
            k_group = g * HID_PASSES + c
            nc.vector.quantize_mx(
                out=h_codes[:, k_group, rows].bitcast(FP8X4),
                scales=h_scales[:, k_group, rows],
                in_=h_grouped[:].rearrange("p b t -> p (b t)"),
            )

        def layer2_bank(tag, bufs):
            return psum.tile([P, LANE_GROUP, FEAT_CHUNK], F32, tag=tag, bufs=bufs, name="acc2")

        def layer2(group, r, f, acc2, lanes=range(LANE_GROUP)):
            feats = slice(f * FEAT_CHUNK, (f + 1) * FEAT_CHUNK)
            rows = slice(r * P, (r + 1) * P)
            for m in lanes:
                for c in range(HID_PASSES):
                    k_group = (group * LANE_GROUP + m) * HID_PASSES + c
                    nc.tensor.matmul_mx(
                        out=acc2[:, m, :],
                        lhsT=h_codes[:, k_group, rows].bitcast(FP8X4),
                        lhsT_scale=h_scales[:, k_group, rows],
                        rhs=w2_codes[:, k_group, feats].bitcast(FP8X4),
                        rhs_scale=w2_planes[4 * (k_group % 4) : P, k_group // 4, feats],
                        start=(c == 0),
                        stop=(c == HID_PASSES - 1),
                    )
            return acc2

        def add_layer2(group, r, f, acc2, pieces=1):
            lanes = slice(group * LANE_GROUP, (group + 1) * LANE_GROUP)
            width = FEAT_CHUNK // pieces
            for at in range(0, FEAT_CHUNK, width):
                first_feat = f * FEAT_CHUNK + at
                feats = slice(first_feat, first_feat + width)
                nc.vector.tensor_tensor(
                    out=result[r][:, feats, lanes],
                    in0=acc2[:, :, at : at + width].rearrange("b g d -> b d g"),
                    in1=result[r][:, feats, lanes],
                    op=ALU.add,
                )
                if group == GROUPS - 1:
                    nc.sync.dma_start(
                        out=out[r * P : (r + 1) * P, first_feat * LANES : (first_feat + width) * LANES],
                        in_=result[r][:, feats, :].rearrange("b d g -> b (d g)"),
                    )

        both = slice(0, ROWS)
        tiles = [slice(r * P, (r + 1) * P) for r in range(ROW_TILES)]
        lanes_rows = [(0, tiles[0]), (0, tiles[1])]
        lanes_rows += [(g, both) for g in range(1, LANES - 2)]
        lanes_rows += [(g, tiles[r]) for r in range(ROW_TILES) for g in (LANES - 2, LANES - 1)]
        steps = [(g, c, rows) for g, rows in lanes_rows for c in range(HID_PASSES)]
        first = [min(i for i, s in enumerate(steps) if s[0] == g) for g in range(LANES)]

        def last(group, r):
            return max(
                i
                for i, s in enumerate(steps)
                if s[0] // LANE_GROUP == group and s[2].start <= r * P < s[2].stop
            )

        chunks = [(group, r, f) for group in range(GROUPS) for r in range(ROW_TILES) for f in range(FEAT_CHUNKS)]
        by_scalar = [(0, q) for q in range(6)] + [(1, q) for q in range(5)]

        def steps_are_long(i):
            return i < len(steps) and steps[i][2] == both

        def new_z(width):
            return work.tile([P, WORD_LANES, width, PACK], BF16, tag="z_grouped", bufs=2, align_bytes=64, name="z_grouped")

        warm_up()
        sort_b2()
        z_first = new_z(P)
        copy_z(transpose_z(0, 0), z_first, 0)
        bias_columns()
        for q in range(HEAD_RESIDUALS):
            residual_by_matmul(*by_scalar.pop(0), "acc2")
        quantise_z_tile(0, 0, z_first)
        sort_planes(0, 0)
        sort_codes(0, 0)
        sums = layer1(steps[0])
        sort_planes(0, 1)
        sort_codes(0, 1)
        sums_ahead = layer1(steps[1])
        banks = [(q, spread_b2(q, "acc2")) for q in (6, 7)]
        z_second = new_z(P)
        zt = transpose_z(0, 1)
        parts = exp_and_relu(steps[0], sums, ())
        residual_plus_bias(0, *banks[0])
        h_grouped = elu(steps[0], parts)
        residual_plus_bias(0, *banks[1])
        parts_before = exp_and_relu(steps[1], sums_ahead, ())
        copy_z(zt, z_second, 0)
        residual_by_matmul(*by_scalar.pop(0), "small")
        quantise_z_tile(0, 1, z_second)
        quantise_h(steps[0], h_grouped)
        sums_ahead = layer1(steps[2])
        for q, bank in banks:
            residual_plus_bias(1, q, bank)
        sort_codes(1, 0)
        sort_codes(1, 1)
        z_waiting = None
        sorting = {g: (sort_codes, g) for g in range(2, LANES - 1)}
        sorting[LANES - 1] = (sort_planes, 1)
        sorting[LANES] = (sort_codes, LANES - 1)
        adds = []
        tail = [(GROUPS - 1, ROW_TILES - 1, f) for f in range(FEAT_CHUNKS)]
        chunks = [ch for ch in chunks if ch not in tail]
        tail_banks = []
        for i in range(2, len(steps) + 1):
            sums = sums_ahead
            if i + 1 < len(steps):
                sums_ahead = layer1(steps[i + 1])
            relu_by_vector(parts_before)
            if i >= 3:
                quantise_h(steps[i - 2], h_grouped)
            ready = [ch for ch in chunks if last(ch[0], ch[1]) + 2 <= i]
            for chunk in ready[: 2 if i == len(steps) - 1 else 1]:
                chunks.remove(chunk)
                adds.append((chunk, layer2(*chunk, layer2_bank("acc2", 2))))
            if i == len(steps) - 1:
                for f, chunk in enumerate(tail):
                    bank = layer2_bank("small", 2) if f < 2 else layer2_bank("acc1", 4)
                    tail_banks.append(layer2(*chunk, bank, range(LANE_GROUP - 1)))
            parts = exp_and_relu(steps[i], sums, V_RELU if i in V_STEPS else ()) if i < len(steps) else None
            if by_scalar and i >= SCALAR_FROM:
                residual_by_matmul(*by_scalar.pop(0), "small")
            for j in range(1, PAIRS):
                start = first[j * WORD_LANES] - 4
                if i == start:
                    z_waiting = new_z(ROWS)
                    copy_z(transpose_z(j, 0), z_waiting, 0)
                if i == start + 1:
                    copy_z(transpose_z(j, 1), z_waiting, P)
            h_grouped = elu(steps[i - 1], parts_before)
            parts_before = parts
            for j in range(1, PAIRS):
                if i == first[j * WORD_LANES] - 2:
                    quantise_z(j, z_waiting)
            if i in sorting:
                sort, what = sorting[i]
                for c in range(HID_PASSES):
                    sort(what, c)
            for chunk, acc2 in adds[:1]:
                adds.remove((chunk, acc2))
                add_layer2(*chunk, acc2)
            if i == 2:
                residual_plus_bias(1, 5, spread_b2(5, "small"))
        quantise_h(steps[-1], h_grouped)
        for chunk, bank in zip(tail, tail_banks):
            layer2(*chunk, bank, (LANE_GROUP - 1,))
            add_layer2(*chunk, bank, 2 if chunk == tail[0] else 1)
